import numpy as np
import ml_dtypes


def mxq(x, axis, fmt="e4m3"):
    dtype, down = {"e4m3": (ml_dtypes.float8_e4m3fn, 7), "e5m2": (ml_dtypes.float8_e5m2, 14)}[fmt]
    v = np.moveaxis(np.asarray(x, np.float32).astype(ml_dtypes.bfloat16).astype(np.float64), axis, -1)
    blocks = v.reshape(v.shape[:-1] + (-1, 32))
    amax = np.abs(blocks).max(-1, keepdims=True)
    byte = np.maximum(np.where(amax > 0, np.frexp(amax)[1] - 1 + 127, 0) - down, 1)
    scale = np.exp2(byte - 127.0)
    codes = (blocks / scale).astype(np.float32).astype(dtype).astype(np.float64)
    return np.moveaxis((codes * scale).reshape(v.shape), -1, axis)


WIDE = False


def mx_kscale(k):
    if not WIDE:
        return np.ones(k)
    levels = np.array([10, -10, 5, -5, 0])
    a = np.random.permutation(np.resize(levels, k // 512 * 4)).reshape(k // 512, 4)
    idx = np.arange(k)
    return np.exp2(a[idx // 512, idx % 128 // 32])


BF16 = ml_dtypes.bfloat16


def bf(x):
    return np.asarray(x, np.float32).astype(BF16)


def f64(x):
    return np.asarray(x).astype(np.float64)


B, S, D, H, DH, DV, R = 4, 256, 2048, 16, 128, 128, 512
EPS = 1e-6
ROPE_THETA = 10000.0


def rms_norm(c, w):
    var = np.mean(np.square(c), axis=-1, keepdims=True)
    return c * (1.0 / np.sqrt(var + EPS)) * w


def apply_rope(t, cos, sin):
    b, s, h, d = t.shape
    tr = t.reshape(b, s, h, d // 2, 2)
    x1, x2 = tr[..., 0], tr[..., 1]
    c = cos[None, :, None, :]
    sn = sin[None, :, None, :]
    o1 = x1 * c - x2 * sn
    o2 = x1 * sn + x2 * c
    return np.stack([o1, o2], axis=-1).reshape(b, s, h, d)


def setup_inputs():
    s = mx_kscale(D)
    t = mx_kscale(R)
    inv_freq = 1.0 / ROPE_THETA ** (np.arange(0, DH, 2) / DH)
    ang = np.arange(S)[:, None] * inv_freq[None, :]
    return {"x": bf(np.random.standard_normal((B, S, D)) * s),
            "freqs_cos": bf(np.cos(ang)),
            "freqs_sin": bf(np.sin(ang)),
            "w_kv_compress": bf(np.random.standard_normal((D, R)) / np.sqrt(D) / s[:, None]),
            "kv_norm_w": bf((1.0 + 0.1 * np.random.standard_normal(R)) * t),
            "w_k_up": bf(np.random.standard_normal((R, H * DH)) / np.sqrt(R) / t[:, None]),
            "w_v_up": bf(np.random.standard_normal((R, H * DV)) / np.sqrt(R) / t[:, None])}


def reference(x, freqs_cos, freqs_sin, w_kv_compress, kv_norm_w, w_k_up, w_v_up):
    c = mxq(f64(x), 2, "e4m3") @ mxq(f64(w_kv_compress), 0, "e4m3")
    latent_q = mxq(rms_norm(c, f64(kv_norm_w)), 2, "e4m3")
    k = (latent_q @ mxq(f64(w_k_up), 0, "e4m3")).reshape(B, S, H, DH)
    v = (latent_q @ mxq(f64(w_v_up), 0, "e4m3")).reshape(B, S, H, DV)
    return apply_rope(k, f64(freqs_cos), f64(freqs_sin)), v

@@ -1,0 +1,302 @@
+from contextlib import ExitStack
+
+import concourse.mybir as mybir
+from concourse.masks import make_identity
+
+FP8X4 = mybir.dt.float8_e4m3fn_x4
+BF16 = mybir.dt.bfloat16
+F32 = mybir.dt.float32
+U32 = mybir.dt.uint32
+U8 = mybir.dt.uint8
+ALU = mybir.AluOpType
+ACT = mybir.ActivationFunctionType
+
+P = 128
+PACK = 4
+K_PASS = P * PACK
+TOKENS = 1024
+TOKEN_TILES = TOKENS // P
+D_MODEL = 2048
+PASSES = D_MODEL // K_PASS
+RANK = 512
+OUT_COLS = 2048
+BANK = 512
+CHUNKS = OUT_COLS // BANK
+HEAD = 128
+PAIRS = HEAD // 2
+HEADS = BANK // HEAD
+POSITIONS = 256
+HALVES = POSITIONS // P
+PIECE = 128
+PIECES = 2 * BANK // PIECE
+EPS = 1e-6
+
+FLOPS = 2 * TOKENS * D_MODEL * RANK + 2 * 2 * TOKENS * RANK * OUT_COLS
+
+
+def regroup(copy, grouped, rows):
+    copy(
+        out=grouped.rearrange("p (c i) t -> p c t i", i=4),
+        in_=rows.rearrange("p t (c i) -> p c t i", i=4),
+    )
+
+
+def quantise(nc, grouped, codes, scales):
+    nc.vector.quantize_mx(out=codes.bitcast(FP8X4), scales=scales, in_=grouped)
+
+
+def tile_mla_pa_kernel(
+    tc, x, freqs_cos, freqs_sin, w_kv_compress, kv_norm_w, w_k_up, w_v_up, out_0, out_1
+):
+    nc = tc.nc
+    x_rows = x.flatten_outer_dims()
+    k_rows = out_0.rearrange("b s h d -> (b s) (h d)")
+    v_rows = out_1.rearrange("b s h d -> (b s) (h d)")
+
+    with ExitStack() as stack:
+        keep = stack.enter_context(tc.tile_pool(name="keep", bufs=1))
+        x_pool = stack.enter_context(tc.tile_pool(name="x_pool", bufs=TOKEN_TILES))
+        stage = stack.enter_context(tc.tile_pool(name="stage", bufs=3))
+        outs = stack.enter_context(tc.tile_pool(name="outs", bufs=4))
+        psum = stack.enter_context(tc.psum_pool(name="psum", bufs=4))
+
+        eps = keep.tile([P, 1], F32)
+        nc.vector.memset(eps[:], EPS)
+        table_warmer = keep.tile([P, 1], F32)
+        nc.scalar.sqrt(table_warmer[:], eps[:])
+        ident_f32 = keep.tile([P, P], F32)
+        make_identity(nc, ident_f32[:])
+        ident_bf16 = keep.tile([P, P], BF16)
+        make_identity(nc, ident_bf16[:])
+
+        gain = keep.tile([P, RANK], BF16)
+        nc.scalar.dma_start(out=gain[:], in_=kv_norm_w.partition_broadcast(P))
+        cos_raw = keep.tile([P, HALVES, PAIRS], BF16)
+        nc.scalar.dma_start(out=cos_raw[:], in_=freqs_cos.rearrange("(a p) i -> p a i", p=P))
+        sin_raw = keep.tile([P, HALVES, PAIRS], BF16)
+        nc.scalar.dma_start(out=sin_raw[:], in_=freqs_sin.rearrange("(a p) i -> p a i", p=P))
+
+        x_raw = []
+
+        def load_tokens(m):
+            tokens = x_pool.tile([P, D_MODEL], BF16)
+            nc.sync.dma_start(out=tokens[:], in_=x_rows[m * P : (m + 1) * P, :])
+            x_raw.append(tokens)
+
+        wc_raw = keep.tile([P, PASSES, PACK, RANK], BF16)
+
+        def load_compress(g):
+            nc.sync.dma_start(
+                out=wc_raw[:, g].rearrange("p (u e) c -> p u e c", e=2),
+                in_=w_kv_compress[g * K_PASS : (g + 1) * K_PASS, :].rearrange(
+                    "(u q e) c -> q u e c", u=2, e=2
+                ),
+            )
+
+        wk_raw = keep.tile([P, PACK, OUT_COLS], BF16)
+        wv_raw = keep.tile([P, PACK, OUT_COLS], BF16)
+
+        def load_up(raw, weight, half):
+            cols = slice(half * OUT_COLS // 2, (half + 1) * OUT_COLS // 2)
+            nc.sync.dma_start(
+                out=raw[:, :, cols], in_=weight.rearrange("(t p) n -> p t n", p=P)[:, :, cols]
+            )
+
+        load_tokens(0)
+        for g in range(PASSES):
+            load_compress(g)
+        load_up(wk_raw, w_k_up, 0)
+        load_tokens(1)
+        load_up(wv_raw, w_v_up, 0)
+        for m in range(2, TOKEN_TILES):
+            load_tokens(m)
+        load_up(wk_raw, w_k_up, 1)
+        load_up(wv_raw, w_v_up, 1)
+
+        cos_pairs = keep.tile([P, HALVES, HEAD], F32)
+        nc.gpsimd.tensor_copy(
+            out=cos_pairs[:].rearrange("p a (i e) -> p a i e", e=2),
+            in_=cos_raw[:].unsqueeze(3).to_broadcast([P, HALVES, PAIRS, 2]),
+        )
+        sin_signed = keep.tile([P, HALVES, 2, PAIRS], F32)
+        nc.gpsimd.tensor_scalar(
+            out=sin_signed[:, :, 0, :], in0=sin_raw[:], scalar1=-1.0, scalar2=0.0,
+            op0=ALU.mult, op1=ALU.add,
+        )
+        nc.gpsimd.tensor_copy(out=sin_signed[:, :, 1, :], in_=sin_raw[:])
+
+        wc_codes = keep.tile([P, PASSES, RANK], U32, align_bytes=64)
+        wc_scales = keep.tile([P, PASSES, RANK], U8, align_bytes=64)
+        for g in range(PASSES):
+            wc_grouped = stage.tile([P, RANK, PACK], BF16, align_bytes=64)
+            regroup(nc.vector.tensor_copy, wc_grouped[:], wc_raw[:, g])
+            quantise(
+                nc, wc_grouped[:].rearrange("p c t -> p (c t)"), wc_codes[:, g, :], wc_scales[:, g, :]
+            )
+
+        wk_codes = keep.tile([P, OUT_COLS], U32, align_bytes=64)
+        wk_scales = keep.tile([P, OUT_COLS], U8, align_bytes=64)
+        wv_codes = keep.tile([P, OUT_COLS], U32, align_bytes=64)
+        wv_scales = keep.tile([P, OUT_COLS], U8, align_bytes=64)
+
+        def prepare_piece(copy, n, j):
+            if j < PIECES // 2:
+                raw, codes, scales = wk_raw, wk_codes, wk_scales
+            else:
+                raw, codes, scales = wv_raw, wv_codes, wv_scales
+            first = n * BANK + (j % (PIECES // 2)) * PIECE
+            cols = slice(first, first + PIECE)
+            up_grouped = stage.tile([P, PIECE, PACK], BF16, align_bytes=64)
+            regroup(copy, up_grouped[:], raw[:, :, cols])
+            quantise(nc, up_grouped[:].rearrange("p c t -> p (c t)"), codes[:, cols], scales[:, cols])
+
+        x_codes = {}
+
+        def tokens_to_codes(m):
+            words = x_raw[m][:].bitcast(F32)
+            x_grouped = stage.tile([P, PASSES, P, PACK], BF16, align_bytes=64)
+            grouped_words = (
+                x_grouped[:]
+                .rearrange("p g r t -> p (g r t)")
+                .bitcast(F32)
+                .rearrange("p (g r u) -> p g r u", g=PASSES, u=2)
+            )
+            blocks = BANK // P
+            for b in range(2 * PASSES // blocks):
+                turned = psum.tile([P, blocks, P], F32, tag="plain")
+                for j in range(blocks):
+                    first = (b * blocks + j) * P
+                    nc.tensor.transpose(turned[:, j, :], words[:, first : first + P], ident_f32[:])
+                nc.scalar.copy(
+                    out=grouped_words[:, 2 * b : 2 * b + 2],
+                    in_=turned[:].rearrange("p (g u) r -> p g r u", u=2),
+                )
+            codes = stage.tile([P, PASSES, P], U32, align_bytes=64)
+            scales = stage.tile([P, PASSES, P], U8, align_bytes=64)
+            quantise(
+                nc,
+                x_grouped[:].rearrange("p g r t -> p (g r t)"),
+                codes[:].rearrange("p g r -> p (g r)"),
+                scales[:].rearrange("p g r -> p (g r)"),
+            )
+            x_codes[m] = (codes, scales)
+
+        latent_rows = {}
+
+        def compress_and_norm(m):
+            codes, scales = x_codes[m]
+            c_acc = psum.tile([P, RANK], F32, tag="sums")
+            for g in range(PASSES):
+                nc.tensor.matmul_mx(
+                    out=c_acc[:],
+                    lhsT=codes[:, g, :].bitcast(FP8X4),
+                    lhsT_scale=scales[:, g, :],
+                    rhs=wc_codes[:, g, :].bitcast(FP8X4),
+                    rhs_scale=wc_scales[:, g, :],
+                    start=(g == 0),
+                    stop=(g == PASSES - 1),
+                )
+            squares = stage.tile([P, RANK], BF16)
+            sum_squares = stage.tile([P, 1], F32)
+            nc.scalar.activation(
+                out=squares[:], in_=c_acc[:], func=ACT.Square, accum_out=sum_squares[:]
+            )
+            rms = stage.tile([P, 1], F32)
+            nc.scalar.activation(
+                out=rms[:], in_=sum_squares[:], func=ACT.Sqrt, bias=eps[:], scale=1.0 / RANK
+            )
+            inv_rms = stage.tile([P, 1], F32)
+            nc.vector.reciprocal(out=inv_rms[:], in_=rms[:])
+            latent = stage.tile([P, RANK], BF16)
+            nc.vector.scalar_tensor_tensor(
+                out=latent[:], in0=c_acc[:], scalar=inv_rms[:], in1=gain[:],
+                op0=ALU.mult, op1=ALU.mult,
+            )
+            latent_rows[m] = latent
+
+        latent_codes = keep.tile([P, TOKEN_TILES, P], U32, align_bytes=64)
+        latent_scales = keep.tile([P, TOKEN_TILES, P], U8, align_bytes=64)
+
+        def latent_to_codes(m):
+            latent = latent_rows[m]
+            turned_latent = psum.tile([P, PACK, P], BF16, tag="plain")
+            for t in range(PACK):
+                nc.tensor.transpose(
+                    turned_latent[:, t, :], latent[:, t * P : (t + 1) * P], ident_bf16[:]
+                )
+            latent_grouped = stage.tile([P, P, PACK], BF16, align_bytes=64)
+            nc.scalar.copy(out=latent_grouped[:], in_=turned_latent[:].rearrange("p t r -> p r t"))
+            quantise(
+                nc,
+                latent_grouped[:].rearrange("p r t -> p (r t)"),
+                latent_codes[:, m, :],
+                latent_scales[:, m, :],
+            )
+
+        def project(n, m):
+            rows = slice(m * P, (m + 1) * P)
+            cols = slice(n * BANK, (n + 1) * BANK)
+            a = m % HALVES
+            k_acc = psum.tile([P, BANK], F32, tag="sums")
+            nc.tensor.matmul_mx(
+                out=k_acc[:],
+                lhsT=latent_codes[:, m, :].bitcast(FP8X4),
+                lhsT_scale=latent_scales[:, m, :],
+                rhs=wk_codes[:, cols].bitcast(FP8X4),
+                rhs_scale=wk_scales[:, cols],
+                start=True,
+                stop=True,
+            )
+            v_acc = psum.tile([P, BANK], F32, tag="plain")
+            nc.tensor.matmul_mx(
+                out=v_acc[:],
+                lhsT=latent_codes[:, m, :].bitcast(FP8X4),
+                lhsT_scale=latent_scales[:, m, :],
+                rhs=wv_codes[:, cols].bitcast(FP8X4),
+                rhs_scale=wv_scales[:, cols],
+                start=True,
+                stop=True,
+            )
+            by_cos = stage.tile([P, HEADS, HEAD], F32)
+            nc.vector.tensor_tensor(
+                out=by_cos[:],
+                in0=k_acc[:].rearrange("p (h d) -> p h d", h=HEADS),
+                in1=cos_pairs[:, a].unsqueeze(1).to_broadcast([P, HEADS, HEAD]),
+                op=ALU.mult,
+            )
+            by_sin = stage.tile([P, 2, HEADS, PAIRS], F32)
+            k_pairs = k_acc[:].rearrange("p (h i e) -> p h i e", h=HEADS, e=2)
+            for e in range(2):
+                nc.vector.tensor_tensor(
+                    out=by_sin[:, e],
+                    in0=k_pairs[:, :, :, 1 - e],
+                    in1=sin_signed[:, a, e].unsqueeze(1).to_broadcast([P, HEADS, PAIRS]),
+                    op=ALU.mult,
+                )
+            k_rot = outs.tile([P, BANK], F32)
+            nc.gpsimd.tensor_tensor(
+                out=k_rot[:].rearrange("p (n e) -> p n e", e=2),
+                in0=by_cos[:].rearrange("p h (i e) -> p (h i) e", e=2),
+                in1=by_sin[:].rearrange("p e h i -> p (h i) e"),
+                op=ALU.add,
+            )
+            nc.sync.dma_start(out=k_rows[rows, cols], in_=k_rot[:])
+            v_out = outs.tile([P, BANK], F32)
+            nc.scalar.copy(out=v_out[:], in_=v_acc[:])
+            nc.sync.dma_start(out=v_rows[rows, cols], in_=v_out[:])
+
+        tokens_to_codes(0)
+        for j in range(PIECES):
+            prepare_piece(nc.scalar.copy, 0, j)
+        for m in range(TOKEN_TILES):
+            compress_and_norm(m)
+            if m + 1 < TOKEN_TILES:
+                tokens_to_codes(m + 1)
+            latent_to_codes(m)
+            project(0, m)
+            prepare_piece(nc.vector.tensor_copy, 1, m)
+        for n in range(1, CHUNKS):
+            for m in range(TOKEN_TILES):
+                project(n, m)
+                if n + 1 < CHUNKS:
+                    prepare_piece(nc.scalar.copy, n + 1, m)

@@ -15,34 +15,22 @@ P = 128
 PACK = 4
 K_PASS = P * PACK
 TOKENS = 1024
-TOKEN_TILES = TOKENS // P
+TILES = TOKENS // P
 D_MODEL = 2048
 PASSES = D_MODEL // K_PASS
 RANK = 512
 OUT_COLS = 2048
 BANK = 512
-CHUNKS = OUT_COLS // BANK
+BANKS = 8
+HALF_COLS = OUT_COLS // 2
 HEAD = 128
 PAIRS = HEAD // 2
-HEADS = BANK // HEAD
+HEADS = HALF_COLS // HEAD
 POSITIONS = 256
-HALVES = POSITIONS // P
-PIECE = 128
-PIECES = 2 * BANK // PIECE
+PHASES = POSITIONS // P
 EPS = 1e-6
 
 FLOPS = 2 * TOKENS * D_MODEL * RANK + 2 * 2 * TOKENS * RANK * OUT_COLS
-
-
-def regroup(copy, grouped, rows):
-    copy(
-        out=grouped.rearrange("p (c i) t -> p c t i", i=4),
-        in_=rows.rearrange("p t (c i) -> p c t i", i=4),
-    )
-
-
-def quantise(nc, grouped, codes, scales):
-    nc.vector.quantize_mx(out=codes.bitcast(FP8X4), scales=scales, in_=grouped)
 
 
 def tile_mla_pa_kernel(
@@ -52,251 +40,382 @@ def tile_mla_pa_kernel(
     x_rows = x.flatten_outer_dims()
     k_rows = out_0.rearrange("b s h d -> (b s) (h d)")
     v_rows = out_1.rearrange("b s h d -> (b s) (h d)")
+    scalar_copy = nc.scalar.copy
+    vector_copy = nc.vector.tensor_copy
 
     with ExitStack() as stack:
         keep = stack.enter_context(tc.tile_pool(name="keep", bufs=1))
-        x_pool = stack.enter_context(tc.tile_pool(name="x_pool", bufs=TOKEN_TILES))
         stage = stack.enter_context(tc.tile_pool(name="stage", bufs=3))
         outs = stack.enter_context(tc.tile_pool(name="outs", bufs=4))
-        psum = stack.enter_context(tc.psum_pool(name="psum", bufs=4))
+        psum = stack.enter_context(tc.psum_pool(name="psum", bufs=1))
+        stack.enter_context(tc.manual_schedule())
+
+        banks_used = [0]
+
+        def next_bank():
+            number = banks_used[0] % BANKS
+            banks_used[0] += 1
+            return psum.tile([P, BANK], F32, name="bank%d" % number)
 
         eps = keep.tile([P, 1], F32)
         nc.vector.memset(eps[:], EPS)
         table_warmer = keep.tile([P, 1], F32)
         nc.scalar.sqrt(table_warmer[:], eps[:])
-        ident_f32 = keep.tile([P, P], F32)
-        make_identity(nc, ident_f32[:])
-        ident_bf16 = keep.tile([P, P], BF16)
-        make_identity(nc, ident_bf16[:])
+        ident = keep.tile([P, P], F32)
+        make_identity(nc, ident[:])
+        ones = keep.tile([P, P], BF16)
+        nc.vector.memset(ones[:], 1.0)
+        gain_row = keep.tile([P, RANK], BF16)
+        nc.vector.memset(gain_row[:], 0.0)
 
-        gain = keep.tile([P, RANK], BF16)
-        nc.scalar.dma_start(out=gain[:], in_=kv_norm_w.partition_broadcast(P))
-        cos_raw = keep.tile([P, HALVES, PAIRS], BF16)
+        cos_raw = keep.tile([P, PHASES, PAIRS], BF16)
         nc.scalar.dma_start(out=cos_raw[:], in_=freqs_cos.rearrange("(a p) i -> p a i", p=P))
-        sin_raw = keep.tile([P, HALVES, PAIRS], BF16)
+        sin_raw = keep.tile([P, PHASES, PAIRS], BF16)
         nc.scalar.dma_start(out=sin_raw[:], in_=freqs_sin.rearrange("(a p) i -> p a i", p=P))
 
-        x_raw = []
+        x_raw = {}
+        wc_raw = {}
+        up_raw = {}
 
         def load_tokens(m):
-            tokens = x_pool.tile([P, D_MODEL], BF16)
-            nc.sync.dma_start(out=tokens[:], in_=x_rows[m * P : (m + 1) * P, :])
-            x_raw.append(tokens)
-
-        wc_raw = keep.tile([P, PASSES, PACK, RANK], BF16)
+            x_raw[m] = keep.tile([P, D_MODEL], BF16, name="x_raw%d" % m)
+            nc.sync.dma_start(out=x_raw[m][:], in_=x_rows[m * P : (m + 1) * P, :])
 
         def load_compress(g):
+            wc_raw[g] = keep.tile([P, PACK, RANK], BF16, name="wc_raw%d" % g)
             nc.sync.dma_start(
-                out=wc_raw[:, g].rearrange("p (u e) c -> p u e c", e=2),
+                out=wc_raw[g][:].rearrange("p (u e) c -> p u e c", e=2),
                 in_=w_kv_compress[g * K_PASS : (g + 1) * K_PASS, :].rearrange(
                     "(u q e) c -> q u e c", u=2, e=2
                 ),
             )
 
-        wk_raw = keep.tile([P, PACK, OUT_COLS], BF16)
-        wv_raw = keep.tile([P, PACK, OUT_COLS], BF16)
-
-        def load_up(raw, weight, half):
-            cols = slice(half * OUT_COLS // 2, (half + 1) * OUT_COLS // 2)
-            nc.sync.dma_start(
-                out=raw[:, :, cols], in_=weight.rearrange("(t p) n -> p t n", p=P)[:, :, cols]
-            )
+        def load_up(kind, weight, h):
+            up_raw[kind, h] = keep.tile([P, PACK, HALF_COLS], BF16, name="%s_raw%d" % (kind, h))
+            for u in range(2):
+                nc.sync.dma_start(
+                    out=up_raw[kind, h][:, 2 * u : 2 * u + 2, :],
+                    in_=weight[
+                        u * 2 * P : (u + 1) * 2 * P, h * HALF_COLS : (h + 1) * HALF_COLS
+                    ].rearrange("(q e) c -> q e c", e=2),
+                )
 
         load_tokens(0)
+        nc.sync.dma_start(out=gain_row[0:1, :], in_=kv_norm_w.unsqueeze(0))
         for g in range(PASSES):
             load_compress(g)
-        load_up(wk_raw, w_k_up, 0)
         load_tokens(1)
-        load_up(wv_raw, w_v_up, 0)
-        for m in range(2, TOKEN_TILES):
+        load_up("k", w_k_up, 0)
+        load_tokens(2)
+        load_up("v", w_v_up, 0)
+        for m in range(3, TILES):
             load_tokens(m)
-        load_up(wk_raw, w_k_up, 1)
-        load_up(wv_raw, w_v_up, 1)
+        load_up("k", w_k_up, 1)
+        load_up("v", w_v_up, 1)
 
-        cos_pairs = keep.tile([P, HALVES, HEAD], F32)
-        nc.gpsimd.tensor_copy(
-            out=cos_pairs[:].rearrange("p a (i e) -> p a i e", e=2),
-            in_=cos_raw[:].unsqueeze(3).to_broadcast([P, HALVES, PAIRS, 2]),
+        sin_less_cos = keep.tile([P, PHASES, PAIRS], F32)
+        nc.gpsimd.tensor_tensor(
+            out=sin_less_cos[:], in0=sin_raw[:], in1=cos_raw[:], op=ALU.subtract
         )
-        sin_signed = keep.tile([P, HALVES, 2, PAIRS], F32)
+        cos_plus_sin = keep.tile([P, PHASES, PAIRS], F32)
+        nc.gpsimd.tensor_tensor(out=cos_plus_sin[:], in0=sin_raw[:], in1=cos_raw[:], op=ALU.add)
+        minus_sum = keep.tile([P, PHASES, PAIRS], F32)
         nc.gpsimd.tensor_scalar(
-            out=sin_signed[:, :, 0, :], in0=sin_raw[:], scalar1=-1.0, scalar2=0.0,
+            out=minus_sum[:], in0=cos_plus_sin[:], scalar1=-1.0, scalar2=0.0,
             op0=ALU.mult, op1=ALU.add,
         )
-        nc.gpsimd.tensor_copy(out=sin_signed[:, :, 1, :], in_=sin_raw[:])
 
-        wc_codes = keep.tile([P, PASSES, RANK], U32, align_bytes=64)
-        wc_scales = keep.tile([P, PASSES, RANK], U8, align_bytes=64)
-        for g in range(PASSES):
-            wc_grouped = stage.tile([P, RANK, PACK], BF16, align_bytes=64)
-            regroup(nc.vector.tensor_copy, wc_grouped[:], wc_raw[:, g])
-            quantise(
-                nc, wc_grouped[:].rearrange("p c t -> p (c t)"), wc_codes[:, g, :], wc_scales[:, g, :]
+        grouped_panel = {}
+        panels = {}
+
+        def panel_source(panel):
+            kind, h, part = panel
+            if kind == "c":
+                return wc_raw[h][:]
+            if kind == "v":
+                return up_raw["v", h][:, :, part * BANK : (part + 1) * BANK]
+            return up_raw["k", h][:].rearrange("p t (n e) -> p t n e", e=2)[:, :, :, part]
+
+        def regroup(panel, side, copy):
+            if panel not in grouped_panel:
+                grouped_panel[panel] = stage.tile(
+                    [P, BANK, PACK], BF16, name="grouped", align_bytes=64, bufs=4
+                )
+            cols = slice(side * BANK // 2, (side + 1) * BANK // 2)
+            copy(
+                out=grouped_panel[panel][:, cols, :].rearrange("p (c i) t -> p c t i", i=4),
+                in_=panel_source(panel)[:, :, cols].rearrange("p t (c i) -> p c t i", i=4),
             )
 
-        wk_codes = keep.tile([P, OUT_COLS], U32, align_bytes=64)
-        wk_scales = keep.tile([P, OUT_COLS], U8, align_bytes=64)
-        wv_codes = keep.tile([P, OUT_COLS], U32, align_bytes=64)
-        wv_scales = keep.tile([P, OUT_COLS], U8, align_bytes=64)
+        def quantise_panel(panel):
+            name = "%s%d%d" % panel
+            codes = keep.tile([P, BANK], U32, name="codes_" + name, align_bytes=64)
+            scales = keep.tile([P, BANK], U8, name="scales_" + name, align_bytes=64)
+            nc.vector.quantize_mx(
+                out=codes[:].bitcast(FP8X4),
+                scales=scales[:],
+                in_=grouped_panel[panel][:].rearrange("p c t -> p (c t)"),
+            )
+            panels[panel] = (codes, scales)
 
-        def prepare_piece(copy, n, j):
-            if j < PIECES // 2:
-                raw, codes, scales = wk_raw, wk_codes, wk_scales
-            else:
-                raw, codes, scales = wv_raw, wv_codes, wv_scales
-            first = n * BANK + (j % (PIECES // 2)) * PIECE
-            cols = slice(first, first + PIECE)
-            up_grouped = stage.tile([P, PIECE, PACK], BF16, align_bytes=64)
-            regroup(copy, up_grouped[:], raw[:, :, cols])
-            quantise(nc, up_grouped[:].rearrange("p c t -> p (c t)"), codes[:, cols], scales[:, cols])
+        def multiply(out, left, right, start, stop):
+            nc.tensor.matmul_mx(
+                out=out,
+                lhsT=left[0].bitcast(FP8X4),
+                lhsT_scale=left[1],
+                rhs=right[0][:].bitcast(FP8X4),
+                rhs_scale=right[1][:],
+                start=start,
+                stop=stop,
+            )
 
+        x_banks = {}
+        x_grouped = {}
         x_codes = {}
 
-        def tokens_to_codes(m):
+        def turn_tokens(m):
             words = x_raw[m][:].bitcast(F32)
-            x_grouped = stage.tile([P, PASSES, P, PACK], BF16, align_bytes=64)
-            grouped_words = (
-                x_grouped[:]
-                .rearrange("p g r t -> p (g r t)")
-                .bitcast(F32)
-                .rearrange("p (g r u) -> p g r u", g=PASSES, u=2)
-            )
-            blocks = BANK // P
-            for b in range(2 * PASSES // blocks):
-                turned = psum.tile([P, blocks, P], F32, tag="plain")
-                for j in range(blocks):
-                    first = (b * blocks + j) * P
-                    nc.tensor.transpose(turned[:, j, :], words[:, first : first + P], ident_f32[:])
-                nc.scalar.copy(
-                    out=grouped_words[:, 2 * b : 2 * b + 2],
-                    in_=turned[:].rearrange("p (g u) r -> p g r u", u=2),
+            x_banks[m] = []
+            for b in range(2):
+                bank = next_bank()
+                for j in range(4):
+                    first = (4 * b + j) * P
+                    nc.tensor.transpose(
+                        bank[:, j * P : (j + 1) * P], words[:, first : first + P], ident[:]
+                    )
+                x_banks[m].append(bank)
+
+        def empty_tokens(m):
+            x_grouped[m] = stage.tile([P, PASSES * P * PACK], BF16, name="x_grouped", align_bytes=64)
+            words = x_grouped[m][:].bitcast(F32).rearrange("p (b g r u) -> p b g r u", b=2, g=2, u=2)
+            for b in range(2):
+                scalar_copy(
+                    out=words[:, b],
+                    in_=x_banks[m][b][:].rearrange("p (g u r) -> p g r u", g=2, u=2),
                 )
-            codes = stage.tile([P, PASSES, P], U32, align_bytes=64)
-            scales = stage.tile([P, PASSES, P], U8, align_bytes=64)
-            quantise(
-                nc,
-                x_grouped[:].rearrange("p g r t -> p (g r t)"),
-                codes[:].rearrange("p g r -> p (g r)"),
-                scales[:].rearrange("p g r -> p (g r)"),
+
+        def quantise_tokens(m):
+            codes = stage.tile([P, PASSES, P], U32, name="x_codes", align_bytes=64)
+            scales = stage.tile([P, PASSES, P], U8, name="x_scales", align_bytes=64)
+            nc.vector.quantize_mx(
+                out=codes[:].rearrange("p g r -> p (g r)").bitcast(FP8X4),
+                scales=scales[:].rearrange("p g r -> p (g r)"),
+                in_=x_grouped[m][:],
             )
             x_codes[m] = (codes, scales)
 
-        latent_rows = {}
+        c_banks = {}
+        rms_of = {}
+        inv_rms_of = {}
+        latents = {}
 
-        def compress_and_norm(m):
+        def compress(m):
             codes, scales = x_codes[m]
-            c_acc = psum.tile([P, RANK], F32, tag="sums")
+            c_banks[m] = next_bank()
             for g in range(PASSES):
-                nc.tensor.matmul_mx(
-                    out=c_acc[:],
-                    lhsT=codes[:, g, :].bitcast(FP8X4),
-                    lhsT_scale=scales[:, g, :],
-                    rhs=wc_codes[:, g, :].bitcast(FP8X4),
-                    rhs_scale=wc_scales[:, g, :],
-                    start=(g == 0),
-                    stop=(g == PASSES - 1),
+                multiply(
+                    c_banks[m][:], (codes[:, g, :], scales[:, g, :]), panels["c", g, 0],
+                    g == 0, g == PASSES - 1,
                 )
-            squares = stage.tile([P, RANK], BF16)
-            sum_squares = stage.tile([P, 1], F32)
+
+        def root_mean_square(m):
+            squares = stage.tile([P, RANK], BF16, name="squares")
+            sum_squares = stage.tile([P, 1], F32, name="sum_squares")
             nc.scalar.activation(
-                out=squares[:], in_=c_acc[:], func=ACT.Square, accum_out=sum_squares[:]
+                out=squares[:], in_=c_banks[m][:], func=ACT.Square, accum_out=sum_squares[:]
             )
-            rms = stage.tile([P, 1], F32)
+            rms_of[m] = stage.tile([P, 1], F32, name="rms")
             nc.scalar.activation(
-                out=rms[:], in_=sum_squares[:], func=ACT.Sqrt, bias=eps[:], scale=1.0 / RANK
+                out=rms_of[m][:], in_=sum_squares[:], func=ACT.Sqrt, bias=eps[:], scale=1.0 / RANK
             )
-            inv_rms = stage.tile([P, 1], F32)
-            nc.vector.reciprocal(out=inv_rms[:], in_=rms[:])
-            latent = stage.tile([P, RANK], BF16)
+
+        def invert(m):
+            inv_rms_of[m] = stage.tile([P, 1], F32, name="inv_rms")
+            nc.vector.reciprocal(out=inv_rms_of[m][:], in_=rms_of[m][:])
+
+        def normalise(m):
+            latents[m] = stage.tile([P, RANK], BF16, name="latent")
             nc.vector.scalar_tensor_tensor(
-                out=latent[:], in0=c_acc[:], scalar=inv_rms[:], in1=gain[:],
+                out=latents[m][:], in0=c_banks[m][:], scalar=inv_rms_of[m][:], in1=gain[:],
                 op0=ALU.mult, op1=ALU.mult,
             )
-            latent_rows[m] = latent
 
-        latent_codes = keep.tile([P, TOKEN_TILES, P], U32, align_bytes=64)
-        latent_scales = keep.tile([P, TOKEN_TILES, P], U8, align_bytes=64)
+        latent_banks = {}
+        latent_grouped = {}
+        latent_codes = {}
 
-        def latent_to_codes(m):
-            latent = latent_rows[m]
-            turned_latent = psum.tile([P, PACK, P], BF16, tag="plain")
-            for t in range(PACK):
+        def turn_latent(m):
+            words = latents[m][:].bitcast(F32)
+            latent_banks[m] = next_bank()
+            for u in range(2):
                 nc.tensor.transpose(
-                    turned_latent[:, t, :], latent[:, t * P : (t + 1) * P], ident_bf16[:]
+                    latent_banks[m][:, u * P : (u + 1) * P], words[:, u * P : (u + 1) * P], ident[:]
                 )
-            latent_grouped = stage.tile([P, P, PACK], BF16, align_bytes=64)
-            nc.scalar.copy(out=latent_grouped[:], in_=turned_latent[:].rearrange("p t r -> p r t"))
-            quantise(
-                nc,
-                latent_grouped[:].rearrange("p r t -> p (r t)"),
-                latent_codes[:, m, :],
-                latent_scales[:, m, :],
+
+        def empty_latent(m):
+            latent_grouped[m] = stage.tile([P, P * PACK], BF16, name="latent_grouped", align_bytes=64)
+            scalar_copy(
+                out=latent_grouped[m][:].bitcast(F32).rearrange("p (r u) -> p r u", u=2),
+                in_=latent_banks[m][:, : 2 * P].rearrange("p (u r) -> p r u", u=2),
             )
 
-        def project(n, m):
-            rows = slice(m * P, (m + 1) * P)
-            cols = slice(n * BANK, (n + 1) * BANK)
-            a = m % HALVES
-            k_acc = psum.tile([P, BANK], F32, tag="sums")
-            nc.tensor.matmul_mx(
-                out=k_acc[:],
-                lhsT=latent_codes[:, m, :].bitcast(FP8X4),
-                lhsT_scale=latent_scales[:, m, :],
-                rhs=wk_codes[:, cols].bitcast(FP8X4),
-                rhs_scale=wk_scales[:, cols],
-                start=True,
-                stop=True,
+        def quantise_latent(m):
+            codes = keep.tile([P, P], U32, name="latent_codes%d" % m, align_bytes=64)
+            scales = keep.tile([P, P], U8, name="latent_scales%d" % m, align_bytes=64)
+            nc.vector.quantize_mx(
+                out=codes[:].bitcast(FP8X4), scales=scales[:], in_=latent_grouped[m][:]
             )
-            v_acc = psum.tile([P, BANK], F32, tag="plain")
-            nc.tensor.matmul_mx(
-                out=v_acc[:],
-                lhsT=latent_codes[:, m, :].bitcast(FP8X4),
-                lhsT_scale=latent_scales[:, m, :],
-                rhs=wv_codes[:, cols].bitcast(FP8X4),
-                rhs_scale=wv_scales[:, cols],
-                start=True,
-                stop=True,
-            )
-            by_cos = stage.tile([P, HEADS, HEAD], F32)
+            latent_codes[m] = (codes[:], scales[:])
+
+        k_banks = {}
+        v_banks = {}
+        by_cos = {}
+        rest = {}
+
+        def project(h, m):
+            left = latent_codes[m]
+            odd, even = panels["k", h, 1], panels["k", h, 0]
+            both_bank, odd_bank, even_bank = next_bank(), next_bank(), next_bank()
+            multiply(both_bank[:], left, odd, True, False)
+            multiply(both_bank[:], left, even, False, True)
+            multiply(odd_bank[:], left, odd, True, True)
+            multiply(even_bank[:], left, even, True, True)
+            k_banks[h, m] = (both_bank, odd_bank, even_bank)
+            v_banks[h, m] = []
+            for part in range(2):
+                bank = next_bank()
+                multiply(bank[:], left, panels["v", h, part], True, True)
+                v_banks[h, m].append(bank)
+
+        def by_table(out, bank, table, m):
             nc.vector.tensor_tensor(
-                out=by_cos[:],
-                in0=k_acc[:].rearrange("p (h d) -> p h d", h=HEADS),
-                in1=cos_pairs[:, a].unsqueeze(1).to_broadcast([P, HEADS, HEAD]),
+                out=out.rearrange("p (h i) -> p h i", h=HEADS),
+                in0=bank[:].rearrange("p (h i) -> p h i", h=HEADS),
+                in1=table[:, m % PHASES].unsqueeze(1).to_broadcast([P, HEADS, PAIRS]),
                 op=ALU.mult,
             )
-            by_sin = stage.tile([P, 2, HEADS, PAIRS], F32)
-            k_pairs = k_acc[:].rearrange("p (h i e) -> p h i e", h=HEADS, e=2)
-            for e in range(2):
-                nc.vector.tensor_tensor(
-                    out=by_sin[:, e],
-                    in0=k_pairs[:, :, :, 1 - e],
-                    in1=sin_signed[:, a, e].unsqueeze(1).to_broadcast([P, HEADS, PAIRS]),
-                    op=ALU.mult,
-                )
-            k_rot = outs.tile([P, BANK], F32)
+
+        def rotate_first(h, m):
+            both_bank, odd_bank, even_bank = k_banks[h, m]
+            by_cos[h, m] = stage.tile([P, BANK], F32, name="by_cos")
+            rest[h, m] = stage.tile([P, 2, BANK], F32, name="rest")
+            by_table(by_cos[h, m][:], both_bank, cos_raw, m)
+            by_table(rest[h, m][:, 0], odd_bank, minus_sum, m)
+
+        def rotate_last(h, m):
+            by_table(rest[h, m][:, 1], k_banks[h, m][2], sin_less_cos, m)
+
+        def add_and_store(h, m):
+            k_out = outs.tile([P, HALF_COLS], F32, name="k_out")
             nc.gpsimd.tensor_tensor(
-                out=k_rot[:].rearrange("p (n e) -> p n e", e=2),
-                in0=by_cos[:].rearrange("p h (i e) -> p (h i) e", e=2),
-                in1=by_sin[:].rearrange("p e h i -> p (h i) e"),
+                out=k_out[:].rearrange("p (n e) -> p n e", e=2),
+                in0=by_cos[h, m][:].unsqueeze(2).to_broadcast([P, BANK, 2]),
+                in1=rest[h, m][:].rearrange("p e n -> p n e"),
                 op=ALU.add,
             )
-            nc.sync.dma_start(out=k_rows[rows, cols], in_=k_rot[:])
-            v_out = outs.tile([P, BANK], F32)
-            nc.scalar.copy(out=v_out[:], in_=v_acc[:])
-            nc.sync.dma_start(out=v_rows[rows, cols], in_=v_out[:])
+            nc.sync.dma_start(
+                out=k_rows[m * P : (m + 1) * P, h * HALF_COLS : (h + 1) * HALF_COLS], in_=k_out[:]
+            )
 
-        tokens_to_codes(0)
-        for j in range(PIECES):
-            prepare_piece(nc.scalar.copy, 0, j)
-        for m in range(TOKEN_TILES):
-            compress_and_norm(m)
-            if m + 1 < TOKEN_TILES:
-                tokens_to_codes(m + 1)
-            latent_to_codes(m)
-            project(0, m)
-            prepare_piece(nc.vector.tensor_copy, 1, m)
-        for n in range(1, CHUNKS):
-            for m in range(TOKEN_TILES):
-                project(n, m)
-                if n + 1 < CHUNKS:
-                    prepare_piece(nc.scalar.copy, n + 1, m)
+        def values(h, m):
+            v_out = outs.tile([P, HALF_COLS], F32, name="v_out")
+            for part in range(2):
+                scalar_copy(
+                    out=v_out[:, part * BANK : (part + 1) * BANK], in_=v_banks[h, m][part][:]
+                )
+            nc.sync.dma_start(
+                out=v_rows[m * P : (m + 1) * P, h * HALF_COLS : (h + 1) * HALF_COLS], in_=v_out[:]
+            )
+
+        compress_panels = [("c", g, 0) for g in range(PASSES)]
+        up_panels = {
+            h: [("k", h, 1), ("k", h, 0), ("v", h, 0), ("v", h, 1)] for h in range(2)
+        }
+        a0, a1, a2, a3 = up_panels[0]
+
+        turn_tokens(0)
+        empty_tokens(0)
+        for g in range(2):
+            regroup(compress_panels[g], 0, vector_copy)
+            regroup(compress_panels[g], 1, scalar_copy)
+        quantise_tokens(0)
+        quantise_panel(compress_panels[0])
+        gain_bank = next_bank()
+        nc.tensor.matmul(gain_bank[:], lhsT=ones[:], rhs=gain_row[:], start=True, stop=True)
+        for g in range(2, PASSES):
+            regroup(compress_panels[g], 0, vector_copy)
+            regroup(compress_panels[g], 1, scalar_copy)
+            quantise_panel(compress_panels[g - 1])
+        turn_tokens(1)
+        empty_tokens(1)
+        gain = keep.tile([P, RANK], F32)
+        scalar_copy(out=gain[:], in_=gain_bank[:])
+        regroup(a0, 0, vector_copy)
+        quantise_panel(compress_panels[3])
+        compress(0)
+        regroup(a0, 1, scalar_copy)
+        quantise_tokens(1)
+        regroup(a1, 0, vector_copy)
+        quantise_panel(a0)
+        root_mean_square(0)
+        regroup(a1, 1, scalar_copy)
+        turn_tokens(2)
+        compress(1)
+        empty_tokens(2)
+        invert(0)
+        regroup(a2, 0, vector_copy)
+        quantise_panel(a1)
+        normalise(0)
+        regroup(a2, 1, scalar_copy)
+        quantise_tokens(2)
+        regroup(a3, 0, vector_copy)
+        regroup(a3, 1, vector_copy)
+        quantise_panel(a2)
+
+        late = [(panel, side) for panel in up_panels[1] for side in range(2)]
+        for s in range(TILES + 1):
+            if s < TILES:
+                turn_latent(s)
+            if s + 3 < TILES:
+                turn_tokens(s + 3)
+            if s + 1 < TILES:
+                root_mean_square(s + 1)
+            if s < TILES:
+                empty_latent(s)
+            if s >= 2:
+                rotate_last(0, s - 2)
+            if s + 3 < TILES:
+                empty_tokens(s + 3)
+            if s < TILES:
+                quantise_latent(s)
+            if s + 1 < TILES:
+                invert(s + 1)
+            if s == 0:
+                quantise_panel(a3)
+            elif s % 2 == 1 and s >= 3:
+                quantise_panel(up_panels[1][(s - 3) // 2])
+            if s >= 1 and s <= 8:
+                regroup(late[s - 1][0], late[s - 1][1], vector_copy if s % 2 else scalar_copy)
+            if s + 1 < TILES:
+                normalise(s + 1)
+            if s >= 1:
+                project(0, s - 1)
+            if s + 2 < TILES:
+                compress(s + 2)
+            if s >= 1:
+                rotate_first(0, s - 1)
+            if s + 3 < TILES:
+                quantise_tokens(s + 3)
+            if s >= 1:
+                values(0, s - 1)
+            if s >= 2:
+                add_and_store(0, s - 2)
+        rotate_last(0, TILES - 1)
+        quantise_panel(up_panels[1][3])
+        add_and_store(0, TILES - 1)
+        for m in range(TILES):
+            project(1, m)
+            rotate_first(1, m)
+            rotate_last(1, m)
+            values(1, m)
+            add_and_store(1, m)

@@ -307,7 +307,7 @@ def tile_mla_pa_kernel(
 
         def add_and_store(h, m):
             k_out = outs.tile([P, HALF_COLS], F32, name="k_out")
-            nc.gpsimd.tensor_tensor(
+            nc.vector.tensor_tensor(
                 out=k_out[:].rearrange("p (n e) -> p n e", e=2),
                 in0=by_cos[h, m][:].unsqueeze(2).to_broadcast([P, BANK, 2]),
                 in1=rest[h, m][:].rearrange("p e n -> p n e"),

@@ -50,11 +50,11 @@ def tile_mla_pa_kernel(
         psum = stack.enter_context(tc.psum_pool(name="psum", bufs=1))
         stack.enter_context(tc.manual_schedule())
 
-        banks_used = [0]
+        rings = {"k": [0, 1, 2], "s": [3], "x": [4, 5], "c": [6, 7]}
 
-        def next_bank():
-            number = banks_used[0] % BANKS
-            banks_used[0] += 1
+        def next_bank(use):
+            number = rings[use].pop(0)
+            rings[use].append(number)
             return psum.tile([P, BANK], F32, name="bank%d" % number)
 
         eps = keep.tile([P, 1], F32)
@@ -63,6 +63,8 @@ def tile_mla_pa_kernel(
         nc.scalar.sqrt(table_warmer[:], eps[:])
         ident = keep.tile([P, P], F32)
         make_identity(nc, ident[:])
+        ident_bf16 = keep.tile([P, P], BF16)
+        make_identity(nc, ident_bf16[:])
         ones = keep.tile([P, P], BF16)
         nc.vector.memset(ones[:], 1.0)
         gain_row = keep.tile([P, RANK], BF16)
@@ -100,15 +102,17 @@ def tile_mla_pa_kernel(
                     ].rearrange("(q e) c -> q e c", e=2),
                 )
 
+        load_compress(0)
         load_tokens(0)
-        nc.sync.dma_start(out=gain_row[0:1, :], in_=kv_norm_w.unsqueeze(0))
-        for g in range(PASSES):
+        for g in range(1, PASSES):
             load_compress(g)
         load_tokens(1)
+        nc.sync.dma_start(out=gain_row[0:1, :], in_=kv_norm_w.unsqueeze(0))
         load_up("k", w_k_up, 0)
         load_tokens(2)
+        load_tokens(3)
         load_up("v", w_v_up, 0)
-        for m in range(3, TILES):
+        for m in range(4, TILES):
             load_tokens(m)
         load_up("k", w_k_up, 1)
         load_up("v", w_v_up, 1)
@@ -147,6 +151,28 @@ def tile_mla_pa_kernel(
                 in_=panel_source(panel)[:, :, cols].rearrange("p t (c i) -> p c t i", i=4),
             )
 
+        def regroup_by_product(panel, side):
+            if panel not in grouped_panel:
+                grouped_panel[panel] = stage.tile(
+                    [P, BANK, PACK], BF16, name="grouped", align_bytes=64, bufs=4
+                )
+            number = rings["k"].pop(0)
+            rings["k"].append(number)
+            bank = psum.tile([P, 2 * BANK], BF16, name="bank%d" % number)
+            for j in range(2):
+                cols = slice((2 * side + j) * P, (2 * side + j + 1) * P)
+                nc.tensor.matmul(
+                    bank[:, j * BANK : (j + 1) * BANK],
+                    lhsT=ident_bf16[:],
+                    rhs=panel_source(panel)[:, :, cols].rearrange("p t c -> p c t"),
+                    start=True,
+                    stop=True,
+                )
+            cols = slice(2 * side * P, 2 * (side + 1) * P)
+            scalar_copy(
+                out=grouped_panel[panel][:, cols, :].rearrange("p c t -> p (c t)"), in_=bank[:]
+            )
+
         def quantise_panel(panel):
             name = "%s%d%d" % panel
             codes = keep.tile([P, BANK], U32, name="codes_" + name, align_bytes=64)
@@ -177,7 +203,7 @@ def tile_mla_pa_kernel(
             words = x_raw[m][:].bitcast(F32)
             x_banks[m] = []
             for b in range(2):
-                bank = next_bank()
+                bank = next_bank("x")
                 for j in range(4):
                     first = (4 * b + j) * P
                     nc.tensor.transpose(
@@ -205,25 +231,30 @@ def tile_mla_pa_kernel(
             x_codes[m] = (codes, scales)
 
         c_banks = {}
+        sums = {}
         rms_of = {}
         inv_rms_of = {}
         latents = {}
 
         def compress(m):
             codes, scales = x_codes[m]
-            c_banks[m] = next_bank()
+            c_banks[m] = next_bank("c")
             for g in range(PASSES):
                 multiply(
                     c_banks[m][:], (codes[:, g, :], scales[:, g, :]), panels["c", g, 0],
                     g == 0, g == PASSES - 1,
                 )
 
-        def root_mean_square(m):
+        def sum_up_squares(m):
             squares = stage.tile([P, RANK], BF16, name="squares")
             sum_squares = stage.tile([P, 1], F32, name="sum_squares")
             nc.scalar.activation(
                 out=squares[:], in_=c_banks[m][:], func=ACT.Square, accum_out=sum_squares[:]
             )
+            sums[m] = sum_squares
+
+        def take_root(m):
+            sum_squares = sums[m]
             rms_of[m] = stage.tile([P, 1], F32, name="rms")
             nc.scalar.activation(
                 out=rms_of[m][:], in_=sum_squares[:], func=ACT.Sqrt, bias=eps[:], scale=1.0 / RANK
@@ -232,6 +263,13 @@ def tile_mla_pa_kernel(
         def invert(m):
             inv_rms_of[m] = stage.tile([P, 1], F32, name="inv_rms")
             nc.vector.reciprocal(out=inv_rms_of[m][:], in_=rms_of[m][:])
+
+        gain = keep.tile([P, RANK], F32)
+
+        def spread_gain():
+            bank = next_bank("k")
+            nc.tensor.matmul(bank[:], lhsT=ones[:], rhs=gain_row[:], start=True, stop=True)
+            scalar_copy(out=gain[:], in_=bank[:])
 
         def normalise(m):
             latents[m] = stage.tile([P, RANK], BF16, name="latent")
@@ -246,7 +284,7 @@ def tile_mla_pa_kernel(
 
         def turn_latent(m):
             words = latents[m][:].bitcast(F32)
-            latent_banks[m] = next_bank()
+            latent_banks[m] = next_bank("s")
             for u in range(2):
                 nc.tensor.transpose(
                     latent_banks[m][:, u * P : (u + 1) * P], words[:, u * P : (u + 1) * P], ident[:]
@@ -272,20 +310,22 @@ def tile_mla_pa_kernel(
         by_cos = {}
         rest = {}
 
-        def project(h, m):
-            left = latent_codes[m]
-            odd, even = panels["k", h, 1], panels["k", h, 0]
-            both_bank, odd_bank, even_bank = next_bank(), next_bank(), next_bank()
-            multiply(both_bank[:], left, odd, True, False)
-            multiply(both_bank[:], left, even, False, True)
-            multiply(odd_bank[:], left, odd, True, True)
-            multiply(even_bank[:], left, even, True, True)
-            k_banks[h, m] = (both_bank, odd_bank, even_bank)
-            v_banks[h, m] = []
-            for part in range(2):
-                bank = next_bank()
-                multiply(bank[:], left, panels["v", h, part], True, True)
-                v_banks[h, m].append(bank)
+        def project_both(h, m):
+            k_banks["both", h, m] = next_bank("k")
+            multiply(k_banks["both", h, m][:], latent_codes[m], panels["k", h, 1], True, False)
+            multiply(k_banks["both", h, m][:], latent_codes[m], panels["k", h, 0], False, True)
+
+        def project_odd(h, m):
+            k_banks["odd", h, m] = next_bank("k")
+            multiply(k_banks["odd", h, m][:], latent_codes[m], panels["k", h, 1], True, True)
+
+        def project_even(h, m):
+            k_banks["even", h, m] = next_bank("k")
+            multiply(k_banks["even", h, m][:], latent_codes[m], panels["k", h, 0], True, True)
+
+        def project_v(h, m, part):
+            v_banks[h, m, part] = next_bank("x")
+            multiply(v_banks[h, m, part][:], latent_codes[m], panels["v", h, part], True, True)
 
         def by_table(out, bank, table, m):
             nc.vector.tensor_tensor(
@@ -295,19 +335,20 @@ def tile_mla_pa_kernel(
                 op=ALU.mult,
             )
 
-        def rotate_first(h, m):
-            both_bank, odd_bank, even_bank = k_banks[h, m]
-            by_cos[h, m] = stage.tile([P, BANK], F32, name="by_cos")
-            rest[h, m] = stage.tile([P, 2, BANK], F32, name="rest")
-            by_table(by_cos[h, m][:], both_bank, cos_raw, m)
-            by_table(rest[h, m][:, 0], odd_bank, minus_sum, m)
+        def rotate_both(h, m):
+            by_cos[h, m] = stage.tile([P, BANK], F32, name="by_cos", bufs=4)
+            by_table(by_cos[h, m][:], k_banks["both", h, m], cos_raw, m)
 
-        def rotate_last(h, m):
-            by_table(rest[h, m][:, 1], k_banks[h, m][2], sin_less_cos, m)
+        def rotate_odd(h, m):
+            rest[h, m] = stage.tile([P, 2, BANK], F32, name="rest", bufs=4)
+            by_table(rest[h, m][:, 0], k_banks["odd", h, m], minus_sum, m)
 
-        def add_and_store(h, m):
+        def rotate_even(h, m):
+            by_table(rest[h, m][:, 1], k_banks["even", h, m], sin_less_cos, m)
+
+        def add_and_store(h, m, engine):
             k_out = outs.tile([P, HALF_COLS], F32, name="k_out")
-            nc.vector.tensor_tensor(
+            engine.tensor_tensor(
                 out=k_out[:].rearrange("p (n e) -> p n e", e=2),
                 in0=by_cos[h, m][:].unsqueeze(2).to_broadcast([P, BANK, 2]),
                 in1=rest[h, m][:].rearrange("p e n -> p n e"),
@@ -317,105 +358,146 @@ def tile_mla_pa_kernel(
                 out=k_rows[m * P : (m + 1) * P, h * HALF_COLS : (h + 1) * HALF_COLS], in_=k_out[:]
             )
 
-        def values(h, m):
-            v_out = outs.tile([P, HALF_COLS], F32, name="v_out")
-            for part in range(2):
-                scalar_copy(
-                    out=v_out[:, part * BANK : (part + 1) * BANK], in_=v_banks[h, m][part][:]
+        v_outs = {}
+
+        def values(h, m, part):
+            if part == 0:
+                v_outs[h, m] = outs.tile([P, HALF_COLS], F32, name="v_out")
+            v_out = v_outs[h, m]
+            scalar_copy(out=v_out[:, part * BANK : (part + 1) * BANK], in_=v_banks[h, m, part][:])
+            if part == 1:
+                nc.scalar.dma_start(
+                    out=v_rows[m * P : (m + 1) * P, h * HALF_COLS : (h + 1) * HALF_COLS], in_=v_out[:]
                 )
-            nc.sync.dma_start(
-                out=v_rows[m * P : (m + 1) * P, h * HALF_COLS : (h + 1) * HALF_COLS], in_=v_out[:]
-            )
 
-        compress_panels = [("c", g, 0) for g in range(PASSES)]
-        up_panels = {
-            h: [("k", h, 1), ("k", h, 0), ("v", h, 0), ("v", h, 1)] for h in range(2)
-        }
-        a0, a1, a2, a3 = up_panels[0]
+        wc = [("c", g, 0) for g in range(PASSES)]
+        up = [(kind, h, part) for h in range(2) for kind, part in (("k", 1), ("k", 0), ("v", 0), ("v", 1))]
 
+        def product(panel, side):
+            regroup_by_product(panel, side)
+
+        def on_vector(panel, side):
+            regroup(panel, side, vector_copy)
+
+        def on_scalar(panel, side):
+            regroup(panel, side, scalar_copy)
+
+        units = [(h, m) for h in range(2) for m in range(TILES)]
+        gpsimd_adds = [(h, m) for h in range(2) for m in range(1, TILES, 2)]
+
+        def add(unit):
+            add_and_store(*unit, nc.gpsimd if unit in gpsimd_adds else nc.vector)
+
+        def extra(s, at):
+            for when, function, panel, sides in work:
+                if when == (s, at):
+                    for side in sides:
+                        if side is None:
+                            function(panel)
+                        else:
+                            function(panel, side)
+
+        q = quantise_panel
+        on_vector(wc[0], 0)
         turn_tokens(0)
         empty_tokens(0)
-        for g in range(2):
-            regroup(compress_panels[g], 0, vector_copy)
-            regroup(compress_panels[g], 1, scalar_copy)
+        on_vector(wc[0], 1)
+        product(wc[1], 1)
+        q(wc[0])
+        on_vector(wc[1], 0)
+        product(wc[2], 1)
         quantise_tokens(0)
-        quantise_panel(compress_panels[0])
-        gain_bank = next_bank()
-        nc.tensor.matmul(gain_bank[:], lhsT=ones[:], rhs=gain_row[:], start=True, stop=True)
-        for g in range(2, PASSES):
-            regroup(compress_panels[g], 0, vector_copy)
-            regroup(compress_panels[g], 1, scalar_copy)
-            quantise_panel(compress_panels[g - 1])
+        on_vector(wc[2], 0)
+        product(wc[3], 1)
+        q(wc[1])
+        on_vector(wc[3], 0)
         turn_tokens(1)
-        empty_tokens(1)
-        gain = keep.tile([P, RANK], F32)
-        scalar_copy(out=gain[:], in_=gain_bank[:])
-        regroup(a0, 0, vector_copy)
-        quantise_panel(compress_panels[3])
+        q(wc[2])
+        spread_gain()
+        q(wc[3])
         compress(0)
-        regroup(a0, 1, scalar_copy)
-        quantise_tokens(1)
-        regroup(a1, 0, vector_copy)
-        quantise_panel(a0)
-        root_mean_square(0)
-        regroup(a1, 1, scalar_copy)
-        turn_tokens(2)
-        compress(1)
-        empty_tokens(2)
-        invert(0)
-        regroup(a2, 0, vector_copy)
-        quantise_panel(a1)
-        normalise(0)
-        regroup(a2, 1, scalar_copy)
-        quantise_tokens(2)
-        regroup(a3, 0, vector_copy)
-        regroup(a3, 1, vector_copy)
-        quantise_panel(a2)
+        empty_tokens(1)
+        sum_up_squares(0)
+        take_root(0)
 
-        late = [(panel, side) for panel in up_panels[1] for side in range(2)]
-        for s in range(TILES + 1):
-            if s < TILES:
-                turn_latent(s)
-            if s + 3 < TILES:
-                turn_tokens(s + 3)
+        work = [
+            ((1, 1), on_vector, up[0], (0,)),
+            ((1, 2), product, up[0], (1,)),
+            ((2, 1), on_vector, up[1], (0,)),
+            ((2, 2), product, up[1], (1,)),
+            ((3, 0), q, up[0], (None,)),
+            ((3, 1), on_vector, up[2], (0,)),
+            ((3, 2), product, up[2], (1,)),
+            ((4, 0), q, up[1], (None,)),
+            ((4, 1), on_vector, up[3], (0,)),
+            ((4, 2), product, up[3], (1,)),
+            ((5, 0), q, up[2], (None,)),
+            ((6, 0), q, up[3], (None,)),
+            ((6, 2), on_scalar, up[4], (0,)),
+            ((7, 2), on_scalar, up[4], (1,)),
+            ((8, 2), on_scalar, up[5], (0,)),
+            ((9, 2), on_scalar, up[5], (1,)),
+            ((10, 2), on_scalar, up[6], (0,)),
+            ((11, 2), on_scalar, up[6], (1,)),
+            ((12, 2), on_scalar, up[7], (0,)),
+            ((13, 2), on_scalar, up[7], (1,)),
+            ((9, 0), q, up[4], (None,)),
+            ((11, 0), q, up[5], (None,)),
+            ((13, 0), q, up[6], (None,)),
+            ((15, 0), q, up[7], (None,)),
+
+        ]
+        first_unit = 7
+        for s in range(1, first_unit + len(units) + 1):
+            j = s - first_unit
+            unit = units[j] if 0 <= j < len(units) else None
+            older = units[j - 1] if 1 <= j <= len(units) else None
+            if s == TILES + 2:
+                rings["k"].extend(rings["s"] + rings["c"])
             if s + 1 < TILES:
-                root_mean_square(s + 1)
+                turn_tokens(s + 1)
             if s < TILES:
-                empty_latent(s)
-            if s >= 2:
-                rotate_last(0, s - 2)
-            if s + 3 < TILES:
-                empty_tokens(s + 3)
+                quantise_tokens(s)
+            extra(s, 0)
+            if 0 <= s - 2 < TILES:
+                quantise_latent(s - 2)
+            if s + 1 < TILES:
+                empty_tokens(s + 1)
+            if unit:
+                project_both(*unit)
             if s < TILES:
-                quantise_latent(s)
-            if s + 1 < TILES:
-                invert(s + 1)
-            if s == 0:
-                quantise_panel(a3)
-            elif s % 2 == 1 and s >= 3:
-                quantise_panel(up_panels[1][(s - 3) // 2])
-            if s >= 1 and s <= 8:
-                regroup(late[s - 1][0], late[s - 1][1], vector_copy if s % 2 else scalar_copy)
-            if s + 1 < TILES:
-                normalise(s + 1)
-            if s >= 1:
-                project(0, s - 1)
-            if s + 2 < TILES:
-                compress(s + 2)
-            if s >= 1:
-                rotate_first(0, s - 1)
-            if s + 3 < TILES:
-                quantise_tokens(s + 3)
-            if s >= 1:
-                values(0, s - 1)
-            if s >= 2:
-                add_and_store(0, s - 2)
-        rotate_last(0, TILES - 1)
-        quantise_panel(up_panels[1][3])
-        add_and_store(0, TILES - 1)
-        for m in range(TILES):
-            project(1, m)
-            rotate_first(1, m)
-            rotate_last(1, m)
-            values(1, m)
-            add_and_store(1, m)
+                compress(s)
+            extra(s, 1)
+            if s - 1 < TILES:
+                invert(s - 1)
+            if unit:
+                project_odd(*unit)
+                project_even(*unit)
+                rotate_both(*unit)
+            if s - 1 < TILES:
+                normalise(s - 1)
+                turn_latent(s - 1)
+            if unit:
+                rotate_odd(*unit)
+            if older and older not in gpsimd_adds:
+                add(older)
+            if unit:
+                rotate_even(*unit)
+                if unit in gpsimd_adds:
+                    add(unit)
+            if s < TILES:
+                sum_up_squares(s)
+                take_root(s)
+            if s - 1 < TILES:
+                empty_latent(s - 1)
+            vu = units[j - 1] if 0 <= j - 1 < len(units) else None
+            if vu:
+                project_v(*vu, 0)
+                values(*vu, 0)
+                project_v(*vu, 1)
+                values(*vu, 1)
+            extra(s, 2)
+        for vu in units[len(units) + 1 - 1 :]:
+            for part in range(2):
+                project_v(*vu, part)
+                values(*vu, part)

@@ -71,9 +71,7 @@ def tile_mla_pa_kernel(
         nc.vector.memset(gain_row[:], 0.0)
 
         cos_raw = keep.tile([P, PHASES, PAIRS], BF16)
-        nc.scalar.dma_start(out=cos_raw[:], in_=freqs_cos.rearrange("(a p) i -> p a i", p=P))
         sin_raw = keep.tile([P, PHASES, PAIRS], BF16)
-        nc.scalar.dma_start(out=sin_raw[:], in_=freqs_sin.rearrange("(a p) i -> p a i", p=P))
 
         x_raw = {}
         wc_raw = {}
@@ -108,8 +106,10 @@ def tile_mla_pa_kernel(
             load_compress(g)
         load_tokens(1)
         nc.sync.dma_start(out=gain_row[0:1, :], in_=kv_norm_w.unsqueeze(0))
-        load_up("k", w_k_up, 0)
         load_tokens(2)
+        nc.sync.dma_start(out=cos_raw[:], in_=freqs_cos.rearrange("(a p) i -> p a i", p=P))
+        nc.sync.dma_start(out=sin_raw[:], in_=freqs_sin.rearrange("(a p) i -> p a i", p=P))
+        load_up("k", w_k_up, 0)
         load_tokens(3)
         load_up("v", w_v_up, 0)
         for m in range(4, TILES):
@@ -140,11 +140,15 @@ def tile_mla_pa_kernel(
                 return up_raw["v", h][:, :, part * BANK : (part + 1) * BANK]
             return up_raw["k", h][:].rearrange("p t (n e) -> p t n e", e=2)[:, :, :, part]
 
-        def regroup(panel, side, copy):
+        def grouped_tile(panel):
             if panel not in grouped_panel:
                 grouped_panel[panel] = stage.tile(
                     [P, BANK, PACK], BF16, name="grouped", align_bytes=64, bufs=4
                 )
+            return grouped_panel[panel]
+
+        def regroup(panel, side, copy):
+            grouped_tile(panel)
             cols = slice(side * BANK // 2, (side + 1) * BANK // 2)
             copy(
                 out=grouped_panel[panel][:, cols, :].rearrange("p (c i) t -> p c t i", i=4),
@@ -152,10 +156,7 @@ def tile_mla_pa_kernel(
             )
 
         def regroup_by_product(panel, side):
-            if panel not in grouped_panel:
-                grouped_panel[panel] = stage.tile(
-                    [P, BANK, PACK], BF16, name="grouped", align_bytes=64, bufs=4
-                )
+            grouped_tile(panel)
             number = rings["k"].pop(0)
             rings["k"].append(number)
             bank = psum.tile([P, 2 * BANK], BF16, name="bank%d" % number)
@@ -346,17 +347,22 @@ def tile_mla_pa_kernel(
         def rotate_even(h, m):
             by_table(rest[h, m][:, 1], k_banks["even", h, m], sin_less_cos, m)
 
-        def add_and_store(h, m, engine):
+        def add_and_store(h, m, engine, parts=1):
             k_out = outs.tile([P, HALF_COLS], F32, name="k_out")
-            engine.tensor_tensor(
-                out=k_out[:].rearrange("p (n e) -> p n e", e=2),
-                in0=by_cos[h, m][:].unsqueeze(2).to_broadcast([P, BANK, 2]),
-                in1=rest[h, m][:].rearrange("p e n -> p n e"),
-                op=ALU.add,
-            )
-            nc.sync.dma_start(
-                out=k_rows[m * P : (m + 1) * P, h * HALF_COLS : (h + 1) * HALF_COLS], in_=k_out[:]
-            )
+            pairs = BANK // parts
+            for part in range(parts):
+                now = slice(part * pairs, (part + 1) * pairs)
+                cols = slice(2 * part * pairs, 2 * (part + 1) * pairs)
+                engine.tensor_tensor(
+                    out=k_out[:, cols].rearrange("p (n e) -> p n e", e=2),
+                    in0=by_cos[h, m][:, now].unsqueeze(2).to_broadcast([P, pairs, 2]),
+                    in1=rest[h, m][:, :, now].rearrange("p e n -> p n e"),
+                    op=ALU.add,
+                )
+                first = h * HALF_COLS + cols.start
+                nc.sync.dma_start(
+                    out=k_rows[m * P : (m + 1) * P, first : first + 2 * pairs], in_=k_out[:, cols]
+                )
 
         v_outs = {}
 
@@ -382,11 +388,22 @@ def tile_mla_pa_kernel(
         def on_scalar(panel, side):
             regroup(panel, side, scalar_copy)
 
+        def on_gpsimd(panel, side):
+            grouped = grouped_tile(panel)
+            for j in range(2):
+                cols = slice((2 * side + j) * P, (2 * side + j + 1) * P)
+                nc.gpsimd.tensor_scalar(
+                    out=grouped[:, cols, :],
+                    in0=panel_source(panel)[:, :, cols].rearrange("p t c -> p c t"),
+                    scalar1=1.0, scalar2=0.0, op0=ALU.mult, op1=ALU.add,
+                )
+
         units = [(h, m) for h in range(2) for m in range(TILES)]
-        gpsimd_adds = [(h, m) for h in range(2) for m in range(1, TILES, 2)]
+        gpsimd_adds = [(h, m) for h in range(2) for m in range(1, TILES, 2) if (h, m) != (1, 7)]
 
         def add(unit):
-            add_and_store(*unit, nc.gpsimd if unit in gpsimd_adds else nc.vector)
+            engine = nc.gpsimd if unit in gpsimd_adds else nc.vector
+            add_and_store(*unit, engine, 2 if unit == units[-1] else 1)
 
         def extra(s, at):
             for when, function, panel, sides in work:
@@ -413,12 +430,12 @@ def tile_mla_pa_kernel(
         on_vector(wc[3], 0)
         turn_tokens(1)
         q(wc[2])
-        spread_gain()
         q(wc[3])
         compress(0)
         empty_tokens(1)
         sum_up_squares(0)
         take_root(0)
+        spread_gain()
 
         work = [
             ((1, 1), on_vector, up[0], (0,)),
@@ -433,18 +450,18 @@ def tile_mla_pa_kernel(
             ((4, 2), product, up[3], (1,)),
             ((5, 0), q, up[2], (None,)),
             ((6, 0), q, up[3], (None,)),
-            ((6, 2), on_scalar, up[4], (0,)),
-            ((7, 2), on_scalar, up[4], (1,)),
-            ((8, 2), on_scalar, up[5], (0,)),
-            ((9, 2), on_scalar, up[5], (1,)),
-            ((10, 2), on_scalar, up[6], (0,)),
+            ((9, 2), product, up[4], (0,)),
+            ((9, 2), on_scalar, up[4], (1,)),
+            ((10, 2), product, up[5], (0,)),
+            ((10, 2), on_scalar, up[5], (1,)),
+            ((11, 2), product, up[6], (0,)),
             ((11, 2), on_scalar, up[6], (1,)),
-            ((12, 2), on_scalar, up[7], (0,)),
+            ((12, 2), product, up[7], (0,)),
             ((13, 2), on_scalar, up[7], (1,)),
-            ((9, 0), q, up[4], (None,)),
-            ((11, 0), q, up[5], (None,)),
-            ((13, 0), q, up[6], (None,)),
-            ((15, 0), q, up[7], (None,)),
+            ((12, 3), q, up[4], (None,)),
+            ((12, 3), q, up[5], (None,)),
+            ((14, 3), q, up[6], (None,)),
+            ((14, 3), q, up[7], (None,)),
 
         ]
         first_unit = 7
@@ -458,6 +475,8 @@ def tile_mla_pa_kernel(
                 turn_tokens(s + 1)
             if s < TILES:
                 quantise_tokens(s)
+            if unit is None and s - 1 < TILES:
+                invert(s - 1)
             extra(s, 0)
             if 0 <= s - 2 < TILES:
                 quantise_latent(s - 2)
@@ -468,7 +487,7 @@ def tile_mla_pa_kernel(
             if s < TILES:
                 compress(s)
             extra(s, 1)
-            if s - 1 < TILES:
+            if unit and s - 1 < TILES:
                 invert(s - 1)
             if unit:
                 project_odd(*unit)
@@ -481,23 +500,20 @@ def tile_mla_pa_kernel(
                 rotate_odd(*unit)
             if older and older not in gpsimd_adds:
                 add(older)
+            extra(s, 3)
             if unit:
                 rotate_even(*unit)
                 if unit in gpsimd_adds:
                     add(unit)
             if s < TILES:
                 sum_up_squares(s)
-                take_root(s)
             if s - 1 < TILES:
                 empty_latent(s - 1)
-            vu = units[j - 1] if 0 <= j - 1 < len(units) else None
-            if vu:
+            if s < TILES:
+                take_root(s)
+            for vu in [u for k, u in enumerate(units) if (k + 1 if k < 8 else k) == j]:
                 project_v(*vu, 0)
                 values(*vu, 0)
                 project_v(*vu, 1)
                 values(*vu, 1)
             extra(s, 2)
-        for vu in units[len(units) + 1 - 1 :]:
-            for part in range(2):
-                project_v(*vu, part)
-                values(*vu, part)

@@ -60,7 +60,7 @@ def tile_mla_pa_kernel(
         eps = keep.tile([P, 1], F32)
         nc.vector.memset(eps[:], EPS)
         table_warmer = keep.tile([P, 1], F32)
-        nc.scalar.sqrt(table_warmer[:], eps[:])
+        nc.scalar.activation(out=table_warmer[:], in_=eps[:], func=ACT.Abs_reciprocal_sqrt)
         ident = keep.tile([P, P], F32)
         make_identity(nc, ident[:])
         ident_bf16 = keep.tile([P, P], BF16)
@@ -130,6 +130,7 @@ def tile_mla_pa_kernel(
         )
 
         grouped_panel = {}
+        grouped_pair = {}
         panels = {}
 
         def panel_source(panel):
@@ -141,15 +142,24 @@ def tile_mla_pa_kernel(
             return up_raw["k", h][:].rearrange("p t (n e) -> p t n e", e=2)[:, :, :, part]
 
         def grouped_tile(panel):
+            kind, h, part = panel
             if panel not in grouped_panel:
-                grouped_panel[panel] = stage.tile(
-                    [P, BANK, PACK], BF16, name="grouped", align_bytes=64, bufs=4
-                )
+                if kind == "c":
+                    grouped_panel[panel] = stage.tile(
+                        [P, BANK, PACK], BF16, name="grouped", align_bytes=64, bufs=3
+                    )[:]
+                else:
+                    pair = stage.tile(
+                        [P, 2, BANK, PACK], BF16, name="grouped_pair", align_bytes=64, bufs=2
+                    )
+                    grouped_pair[kind, h] = pair
+                    for j in range(2):
+                        grouped_panel[kind, h, j] = pair[:, j]
             return grouped_panel[panel]
 
         def regroup(panel, side, copy):
             grouped_tile(panel)
-            cols = slice(side * BANK // 2, (side + 1) * BANK // 2)
+            cols = slice(side * BANK // 2, (side + 1) * BANK // 2) if side < 2 else slice(0, BANK)
             copy(
                 out=grouped_panel[panel][:, cols, :].rearrange("p (c i) t -> p c t i", i=4),
                 in_=panel_source(panel)[:, :, cols].rearrange("p t (c i) -> p c t i", i=4),
@@ -181,17 +191,29 @@ def tile_mla_pa_kernel(
             nc.vector.quantize_mx(
                 out=codes[:].bitcast(FP8X4),
                 scales=scales[:],
-                in_=grouped_panel[panel][:].rearrange("p c t -> p (c t)"),
+                in_=grouped_panel[panel].rearrange("p c t -> p (c t)"),
             )
-            panels[panel] = (codes, scales)
+            panels[panel] = (codes[:], scales[:])
+
+        def quantise_pair(panel):
+            kind, h, part = panel
+            codes = keep.tile([P, 2, BANK], U32, name="codes_%s%d" % (kind, h), align_bytes=64)
+            scales = keep.tile([P, 2, BANK], U8, name="scales_%s%d" % (kind, h), align_bytes=64)
+            nc.vector.quantize_mx(
+                out=codes[:].rearrange("p j c -> p (j c)").bitcast(FP8X4),
+                scales=scales[:].rearrange("p j c -> p (j c)"),
+                in_=grouped_pair[kind, h][:].rearrange("p j c t -> p (j c t)"),
+            )
+            for j in range(2):
+                panels[kind, h, j] = (codes[:, j], scales[:, j])
 
         def multiply(out, left, right, start, stop):
             nc.tensor.matmul_mx(
                 out=out,
                 lhsT=left[0].bitcast(FP8X4),
                 lhsT_scale=left[1],
-                rhs=right[0][:].bitcast(FP8X4),
-                rhs_scale=right[1][:],
+                rhs=right[0].bitcast(FP8X4),
+                rhs_scale=right[1],
                 start=start,
                 stop=stop,
             )
@@ -233,7 +255,6 @@ def tile_mla_pa_kernel(
 
         c_banks = {}
         sums = {}
-        rms_of = {}
         inv_rms_of = {}
         latents = {}
 
@@ -256,14 +277,14 @@ def tile_mla_pa_kernel(
 
         def take_root(m):
             sum_squares = sums[m]
-            rms_of[m] = stage.tile([P, 1], F32, name="rms")
+            inv_rms_of[m] = stage.tile([P, 1], F32, name="inv_rms")
             nc.scalar.activation(
-                out=rms_of[m][:], in_=sum_squares[:], func=ACT.Sqrt, bias=eps[:], scale=1.0 / RANK
+                out=inv_rms_of[m][:], in_=sum_squares[:], func=ACT.Abs_reciprocal_sqrt,
+                bias=eps[:], scale=1.0 / RANK,
             )
 
         def invert(m):
-            inv_rms_of[m] = stage.tile([P, 1], F32, name="inv_rms")
-            nc.vector.reciprocal(out=inv_rms_of[m][:], in_=rms_of[m][:])
+            pass
 
         gain = keep.tile([P, RANK], F32)
 
@@ -415,6 +436,7 @@ def tile_mla_pa_kernel(
                             function(panel, side)
 
         q = quantise_panel
+        qp = quantise_pair
         on_vector(wc[0], 0)
         turn_tokens(0)
         empty_tokens(0)
@@ -438,30 +460,22 @@ def tile_mla_pa_kernel(
         spread_gain()
 
         work = [
-            ((1, 1), on_vector, up[0], (0,)),
-            ((1, 2), product, up[0], (1,)),
-            ((2, 1), on_vector, up[1], (0,)),
-            ((2, 2), product, up[1], (1,)),
-            ((3, 0), q, up[0], (None,)),
-            ((3, 1), on_vector, up[2], (0,)),
-            ((3, 2), product, up[2], (1,)),
-            ((4, 0), q, up[1], (None,)),
-            ((4, 1), on_vector, up[3], (0,)),
-            ((4, 2), product, up[3], (1,)),
-            ((5, 0), q, up[2], (None,)),
-            ((6, 0), q, up[3], (None,)),
-            ((9, 2), product, up[4], (0,)),
-            ((9, 2), on_scalar, up[4], (1,)),
-            ((10, 2), product, up[5], (0,)),
+            ((1, 1), on_vector, up[0], (2,)),
+            ((2, 1), on_vector, up[1], (2,)),
+            ((3, 0), qp, up[0], (None,)),
+            ((4, 1), on_vector, up[2], (2,)),
+            ((5, 1), on_vector, up[3], (2,)),
+            ((6, 0), qp, up[2], (None,)),
+            ((7, 2), on_scalar, up[4], (0,)),
+            ((8, 2), on_scalar, up[4], (1,)),
+            ((9, 2), on_scalar, up[5], (0,)),
             ((10, 2), on_scalar, up[5], (1,)),
-            ((11, 2), product, up[6], (0,)),
-            ((11, 2), on_scalar, up[6], (1,)),
-            ((12, 2), product, up[7], (0,)),
+            ((11, 2), on_scalar, up[6], (0,)),
+            ((12, 2), on_scalar, up[6], (1,)),
+            ((12, 2), on_scalar, up[7], (0,)),
             ((13, 2), on_scalar, up[7], (1,)),
-            ((12, 3), q, up[4], (None,)),
-            ((12, 3), q, up[5], (None,)),
-            ((14, 3), q, up[6], (None,)),
-            ((14, 3), q, up[7], (None,)),
+            ((12, 3), qp, up[4], (None,)),
+            ((14, 3), qp, up[6], (None,)),
 
         ]
         first_unit = 7

@@ -420,7 +420,7 @@ def tile_mla_pa_kernel(
                 )
 
         units = [(h, m) for h in range(2) for m in range(TILES)]
-        gpsimd_adds = [(h, m) for h in range(2) for m in range(1, TILES, 2) if (h, m) != (1, 7)]
+        gpsimd_adds = [u for j, u in enumerate(units) if j % 2 == 1 and j >= 3 and j < 14]
 
         def add(unit):
             engine = nc.gpsimd if unit in gpsimd_adds else nc.vector
@@ -437,6 +437,7 @@ def tile_mla_pa_kernel(
 
         q = quantise_panel
         qp = quantise_pair
+        qp = quantise_pair
         on_vector(wc[0], 0)
         turn_tokens(0)
         empty_tokens(0)
@@ -450,6 +451,7 @@ def tile_mla_pa_kernel(
         product(wc[3], 1)
         q(wc[1])
         on_vector(wc[3], 0)
+        spread_gain()
         turn_tokens(1)
         q(wc[2])
         q(wc[3])
@@ -457,21 +459,24 @@ def tile_mla_pa_kernel(
         empty_tokens(1)
         sum_up_squares(0)
         take_root(0)
-        spread_gain()
 
         work = [
-            ((1, 1), on_vector, up[0], (2,)),
-            ((2, 1), on_vector, up[1], (2,)),
-            ((3, 0), qp, up[0], (None,)),
-            ((4, 1), on_vector, up[2], (2,)),
-            ((5, 1), on_vector, up[3], (2,)),
-            ((6, 0), qp, up[2], (None,)),
-            ((7, 2), on_scalar, up[4], (0,)),
-            ((8, 2), on_scalar, up[4], (1,)),
-            ((9, 2), on_scalar, up[5], (0,)),
-            ((10, 2), on_scalar, up[5], (1,)),
-            ((11, 2), on_scalar, up[6], (0,)),
-            ((12, 2), on_scalar, up[6], (1,)),
+            ((1, 1), on_vector, up[0], (0,)),
+            ((1, 1), on_vector, up[0], (1,)),
+            ((2, 1), on_vector, up[1], (0,)),
+            ((3, 1), on_vector, up[1], (1,)),
+            ((4, 0), qp, up[0], (None,)),
+            ((4, 1), on_vector, up[2], (0,)),
+            ((5, 1), on_vector, up[2], (1,)),
+            ((5, 1), on_vector, up[3], (0,)),
+            ((6, 1), on_vector, up[3], (1,)),
+            ((7, 0), qp, up[2], (None,)),
+            ((6, 2), on_scalar, up[4], (0,)),
+            ((7, 2), on_scalar, up[4], (1,)),
+            ((8, 2), on_scalar, up[5], (0,)),
+            ((9, 2), on_scalar, up[5], (1,)),
+            ((10, 2), on_scalar, up[6], (0,)),
+            ((11, 2), on_scalar, up[6], (1,)),
             ((12, 2), on_scalar, up[7], (0,)),
             ((13, 2), on_scalar, up[7], (1,)),
             ((12, 3), qp, up[4], (None,)),
@@ -512,13 +517,12 @@ def tile_mla_pa_kernel(
                 turn_latent(s - 1)
             if unit:
                 rotate_odd(*unit)
+                rotate_even(*unit)
             if older and older not in gpsimd_adds:
                 add(older)
             extra(s, 3)
-            if unit:
-                rotate_even(*unit)
-                if unit in gpsimd_adds:
-                    add(unit)
+            if unit and unit in gpsimd_adds:
+                add(unit)
             if s < TILES:
                 sum_up_squares(s)
             if s - 1 < TILES:

@@ -462,15 +462,15 @@ def tile_mla_pa_kernel(
 
         work = [
             ((1, 1), on_vector, up[0], (0,)),
-            ((1, 1), on_vector, up[0], (1,)),
+            ((1, 1), on_gpsimd, up[0], (1,)),
             ((2, 1), on_vector, up[1], (0,)),
-            ((3, 1), on_vector, up[1], (1,)),
-            ((4, 0), qp, up[0], (None,)),
-            ((4, 1), on_vector, up[2], (0,)),
-            ((5, 1), on_vector, up[2], (1,)),
-            ((5, 1), on_vector, up[3], (0,)),
-            ((6, 1), on_vector, up[3], (1,)),
-            ((7, 0), qp, up[2], (None,)),
+            ((2, 1), on_gpsimd, up[1], (1,)),
+            ((3, 0), qp, up[0], (None,)),
+            ((3, 1), on_vector, up[2], (0,)),
+            ((3, 1), on_gpsimd, up[2], (1,)),
+            ((4, 1), on_vector, up[3], (0,)),
+            ((4, 1), on_gpsimd, up[3], (1,)),
+            ((6, 0), qp, up[2], (None,)),
             ((6, 2), on_scalar, up[4], (0,)),
             ((7, 2), on_scalar, up[4], (1,)),
             ((8, 2), on_scalar, up[5], (0,)),

@@ -21,7 +21,6 @@ PASSES = D_MODEL // K_PASS
 RANK = 512
 OUT_COLS = 2048
 BANK = 512
-BANKS = 8
 HALF_COLS = OUT_COLS // 2
 HEAD = 128
 PAIRS = HEAD // 2
@@ -32,6 +31,9 @@ EPS = 1e-6
 
 FLOPS = 2 * TOKENS * D_MODEL * RANK + 2 * 2 * TOKENS * RANK * OUT_COLS
 
+FIRST_UNIT_STEP = 7
+SECOND_HALF_STEP = 6
+
 
 def tile_mla_pa_kernel(
     tc, x, freqs_cos, freqs_sin, w_kv_compress, kv_norm_w, w_k_up, w_v_up, out_0, out_1
@@ -40,8 +42,6 @@ def tile_mla_pa_kernel(
     x_rows = x.flatten_outer_dims()
     k_rows = out_0.rearrange("b s h d -> (b s) (h d)")
     v_rows = out_1.rearrange("b s h d -> (b s) (h d)")
-    scalar_copy = nc.scalar.copy
-    vector_copy = nc.vector.tensor_copy
 
     with ExitStack() as stack:
         keep = stack.enter_context(tc.tile_pool(name="keep", bufs=1))
@@ -50,7 +50,7 @@ def tile_mla_pa_kernel(
         psum = stack.enter_context(tc.psum_pool(name="psum", bufs=1))
         stack.enter_context(tc.manual_schedule())
 
-        rings = {"k": [0, 1, 2], "s": [3], "x": [4, 5], "c": [6, 7]}
+        rings = {"k": [0, 1, 2], "turned": [3], "turned x": [4, 5], "c": [6, 7]}
 
         def next_bank(use):
             number = rings[use].pop(0)
@@ -63,15 +63,10 @@ def tile_mla_pa_kernel(
         nc.scalar.activation(out=table_warmer[:], in_=eps[:], func=ACT.Abs_reciprocal_sqrt)
         ident = keep.tile([P, P], F32)
         make_identity(nc, ident[:])
-        ident_bf16 = keep.tile([P, P], BF16)
-        make_identity(nc, ident_bf16[:])
         ones = keep.tile([P, P], BF16)
         nc.vector.memset(ones[:], 1.0)
         gain_row = keep.tile([P, RANK], BF16)
         nc.vector.memset(gain_row[:], 0.0)
-
-        cos_raw = keep.tile([P, PHASES, PAIRS], BF16)
-        sin_raw = keep.tile([P, PHASES, PAIRS], BF16)
 
         x_raw = {}
         wc_raw = {}
@@ -107,8 +102,10 @@ def tile_mla_pa_kernel(
         load_tokens(1)
         nc.sync.dma_start(out=gain_row[0:1, :], in_=kv_norm_w.unsqueeze(0))
         load_tokens(2)
-        nc.sync.dma_start(out=cos_raw[:], in_=freqs_cos.rearrange("(a p) i -> p a i", p=P))
-        nc.sync.dma_start(out=sin_raw[:], in_=freqs_sin.rearrange("(a p) i -> p a i", p=P))
+        cos = keep.tile([P, PHASES, PAIRS], BF16)
+        nc.sync.dma_start(out=cos[:], in_=freqs_cos.rearrange("(a p) i -> p a i", p=P))
+        sin = keep.tile([P, PHASES, PAIRS], BF16)
+        nc.sync.dma_start(out=sin[:], in_=freqs_sin.rearrange("(a p) i -> p a i", p=P))
         load_up("k", w_k_up, 0)
         load_tokens(3)
         load_up("v", w_v_up, 0)
@@ -118,85 +115,69 @@ def tile_mla_pa_kernel(
         load_up("v", w_v_up, 1)
 
         sin_less_cos = keep.tile([P, PHASES, PAIRS], F32)
-        nc.gpsimd.tensor_tensor(
-            out=sin_less_cos[:], in0=sin_raw[:], in1=cos_raw[:], op=ALU.subtract
-        )
+        nc.gpsimd.tensor_tensor(out=sin_less_cos[:], in0=sin[:], in1=cos[:], op=ALU.subtract)
         cos_plus_sin = keep.tile([P, PHASES, PAIRS], F32)
-        nc.gpsimd.tensor_tensor(out=cos_plus_sin[:], in0=sin_raw[:], in1=cos_raw[:], op=ALU.add)
+        nc.gpsimd.tensor_tensor(out=cos_plus_sin[:], in0=sin[:], in1=cos[:], op=ALU.add)
         minus_sum = keep.tile([P, PHASES, PAIRS], F32)
         nc.gpsimd.tensor_scalar(
             out=minus_sum[:], in0=cos_plus_sin[:], scalar1=-1.0, scalar2=0.0,
             op0=ALU.mult, op1=ALU.add,
         )
 
-        grouped_panel = {}
+        grouped = {}
         grouped_pair = {}
         panels = {}
 
         def panel_source(panel):
-            kind, h, part = panel
-            if kind == "c":
-                return wc_raw[h][:]
+            if panel[0] == "c":
+                return wc_raw[panel[1]][:]
+            kind, h, j = panel
             if kind == "v":
-                return up_raw["v", h][:, :, part * BANK : (part + 1) * BANK]
-            return up_raw["k", h][:].rearrange("p t (n e) -> p t n e", e=2)[:, :, :, part]
+                return up_raw["v", h][:, :, j * BANK : (j + 1) * BANK]
+            return up_raw["k", h][:].rearrange("p t (n e) -> p t n e", e=2)[:, :, :, j]
 
         def grouped_tile(panel):
-            kind, h, part = panel
-            if panel not in grouped_panel:
-                if kind == "c":
-                    grouped_panel[panel] = stage.tile(
-                        [P, BANK, PACK], BF16, name="grouped", align_bytes=64, bufs=3
+            if panel not in grouped:
+                if panel[0] == "c":
+                    grouped[panel] = stage.tile(
+                        [P, BANK, PACK], BF16, name="grouped", align_bytes=64
                     )[:]
                 else:
                     pair = stage.tile(
                         [P, 2, BANK, PACK], BF16, name="grouped_pair", align_bytes=64, bufs=2
                     )
-                    grouped_pair[kind, h] = pair
+                    grouped_pair[panel[:2]] = pair
                     for j in range(2):
-                        grouped_panel[kind, h, j] = pair[:, j]
-            return grouped_panel[panel]
+                        grouped[panel[0], panel[1], j] = pair[:, j]
+            return grouped[panel]
 
-        def regroup(panel, side, copy):
-            grouped_tile(panel)
-            cols = slice(side * BANK // 2, (side + 1) * BANK // 2) if side < 2 else slice(0, BANK)
+        first_part, second_part = slice(0, BANK // 2), slice(BANK // 2, BANK)
+
+        def regroup(panel, cols, copy):
             copy(
-                out=grouped_panel[panel][:, cols, :].rearrange("p (c i) t -> p c t i", i=4),
+                out=grouped_tile(panel)[:, cols, :].rearrange("p (c i) t -> p c t i", i=4),
                 in_=panel_source(panel)[:, :, cols].rearrange("p t (c i) -> p c t i", i=4),
             )
 
-        def regroup_by_product(panel, side):
-            grouped_tile(panel)
-            number = rings["k"].pop(0)
-            rings["k"].append(number)
-            bank = psum.tile([P, 2 * BANK], BF16, name="bank%d" % number)
-            for j in range(2):
-                cols = slice((2 * side + j) * P, (2 * side + j + 1) * P)
-                nc.tensor.matmul(
-                    bank[:, j * BANK : (j + 1) * BANK],
-                    lhsT=ident_bf16[:],
-                    rhs=panel_source(panel)[:, :, cols].rearrange("p t c -> p c t"),
-                    start=True,
-                    stop=True,
+        def regroup_on_gpsimd(panel, cols):
+            middle = (cols.start + cols.stop) // 2
+            for now in (slice(cols.start, middle), slice(middle, cols.stop)):
+                nc.gpsimd.tensor_scalar(
+                    out=grouped_tile(panel)[:, now, :],
+                    in0=panel_source(panel)[:, :, now].rearrange("p t c -> p c t"),
+                    scalar1=1.0, scalar2=0.0, op0=ALU.mult, op1=ALU.add,
                 )
-            cols = slice(2 * side * P, 2 * (side + 1) * P)
-            scalar_copy(
-                out=grouped_panel[panel][:, cols, :].rearrange("p c t -> p (c t)"), in_=bank[:]
-            )
 
-        def quantise_panel(panel):
-            name = "%s%d%d" % panel
-            codes = keep.tile([P, BANK], U32, name="codes_" + name, align_bytes=64)
-            scales = keep.tile([P, BANK], U8, name="scales_" + name, align_bytes=64)
+        def quantise_compress(g):
+            codes = keep.tile([P, BANK], U32, name="codes_c%d" % g, align_bytes=64)
+            scales = keep.tile([P, BANK], U8, name="scales_c%d" % g, align_bytes=64)
             nc.vector.quantize_mx(
-                out=codes[:].bitcast(FP8X4),
-                scales=scales[:],
-                in_=grouped_panel[panel].rearrange("p c t -> p (c t)"),
+                out=codes[:].bitcast(FP8X4), scales=scales[:],
+                in_=grouped["c", g].rearrange("p c t -> p (c t)"),
             )
-            panels[panel] = (codes[:], scales[:])
+            panels["c", g] = (codes[:], scales[:])
 
-        def quantise_pair(panel):
-            kind, h, part = panel
+        def quantise_up(kind, h):
             codes = keep.tile([P, 2, BANK], U32, name="codes_%s%d" % (kind, h), align_bytes=64)
             scales = keep.tile([P, 2, BANK], U8, name="scales_%s%d" % (kind, h), align_bytes=64)
             nc.vector.quantize_mx(
@@ -226,7 +207,7 @@ def tile_mla_pa_kernel(
             words = x_raw[m][:].bitcast(F32)
             x_banks[m] = []
             for b in range(2):
-                bank = next_bank("x")
+                bank = next_bank("turned x")
                 for j in range(4):
                     first = (4 * b + j) * P
                     nc.tensor.transpose(
@@ -238,7 +219,7 @@ def tile_mla_pa_kernel(
             x_grouped[m] = stage.tile([P, PASSES * P * PACK], BF16, name="x_grouped", align_bytes=64)
             words = x_grouped[m][:].bitcast(F32).rearrange("p (b g r u) -> p b g r u", b=2, g=2, u=2)
             for b in range(2):
-                scalar_copy(
+                nc.scalar.copy(
                     out=words[:, b],
                     in_=x_banks[m][b][:].rearrange("p (g u r) -> p g r u", g=2, u=2),
                 )
@@ -254,49 +235,43 @@ def tile_mla_pa_kernel(
             x_codes[m] = (codes, scales)
 
         c_banks = {}
-        sums = {}
-        inv_rms_of = {}
+        square_sums = {}
+        inverse_rms = {}
         latents = {}
+        gain = keep.tile([P, RANK], F32)
 
         def compress(m):
             codes, scales = x_codes[m]
             c_banks[m] = next_bank("c")
             for g in range(PASSES):
                 multiply(
-                    c_banks[m][:], (codes[:, g, :], scales[:, g, :]), panels["c", g, 0],
+                    c_banks[m][:], (codes[:, g, :], scales[:, g, :]), panels["c", g],
                     g == 0, g == PASSES - 1,
                 )
 
-        def sum_up_squares(m):
+        def sum_squares(m):
             squares = stage.tile([P, RANK], BF16, name="squares")
-            sum_squares = stage.tile([P, 1], F32, name="sum_squares")
+            square_sums[m] = stage.tile([P, 1], F32, name="square_sums")
             nc.scalar.activation(
-                out=squares[:], in_=c_banks[m][:], func=ACT.Square, accum_out=sum_squares[:]
+                out=squares[:], in_=c_banks[m][:], func=ACT.Square, accum_out=square_sums[m][:]
             )
-            sums[m] = sum_squares
 
-        def take_root(m):
-            sum_squares = sums[m]
-            inv_rms_of[m] = stage.tile([P, 1], F32, name="inv_rms")
+        def invert_rms(m):
+            inverse_rms[m] = stage.tile([P, 1], F32, name="inverse_rms")
             nc.scalar.activation(
-                out=inv_rms_of[m][:], in_=sum_squares[:], func=ACT.Abs_reciprocal_sqrt,
+                out=inverse_rms[m][:], in_=square_sums[m][:], func=ACT.Abs_reciprocal_sqrt,
                 bias=eps[:], scale=1.0 / RANK,
             )
-
-        def invert(m):
-            pass
-
-        gain = keep.tile([P, RANK], F32)
 
         def spread_gain():
             bank = next_bank("k")
             nc.tensor.matmul(bank[:], lhsT=ones[:], rhs=gain_row[:], start=True, stop=True)
-            scalar_copy(out=gain[:], in_=bank[:])
+            nc.scalar.copy(out=gain[:], in_=bank[:])
 
         def normalise(m):
             latents[m] = stage.tile([P, RANK], BF16, name="latent")
             nc.vector.scalar_tensor_tensor(
-                out=latents[m][:], in0=c_banks[m][:], scalar=inv_rms_of[m][:], in1=gain[:],
+                out=latents[m][:], in0=c_banks[m][:], scalar=inverse_rms[m][:], in1=gain[:],
                 op0=ALU.mult, op1=ALU.mult,
             )
 
@@ -306,7 +281,7 @@ def tile_mla_pa_kernel(
 
         def turn_latent(m):
             words = latents[m][:].bitcast(F32)
-            latent_banks[m] = next_bank("s")
+            latent_banks[m] = next_bank("turned")
             for u in range(2):
                 nc.tensor.transpose(
                     latent_banks[m][:, u * P : (u + 1) * P], words[:, u * P : (u + 1) * P], ident[:]
@@ -314,7 +289,7 @@ def tile_mla_pa_kernel(
 
         def empty_latent(m):
             latent_grouped[m] = stage.tile([P, P * PACK], BF16, name="latent_grouped", align_bytes=64)
-            scalar_copy(
+            nc.scalar.copy(
                 out=latent_grouped[m][:].bitcast(F32).rearrange("p (r u) -> p r u", u=2),
                 in_=latent_banks[m][:, : 2 * P].rearrange("p (u r) -> p r u", u=2),
             )
@@ -327,27 +302,22 @@ def tile_mla_pa_kernel(
             )
             latent_codes[m] = (codes[:], scales[:])
 
-        k_banks = {}
-        v_banks = {}
-        by_cos = {}
-        rest = {}
+        both_bank = {}
+        odd_bank = {}
+        even_bank = {}
+        both_product = {}
+        other_products = {}
 
         def project_both(h, m):
-            k_banks["both", h, m] = next_bank("k")
-            multiply(k_banks["both", h, m][:], latent_codes[m], panels["k", h, 1], True, False)
-            multiply(k_banks["both", h, m][:], latent_codes[m], panels["k", h, 0], False, True)
+            both_bank[h, m] = next_bank("k")
+            multiply(both_bank[h, m][:], latent_codes[m], panels["k", h, 1], True, False)
+            multiply(both_bank[h, m][:], latent_codes[m], panels["k", h, 0], False, True)
 
-        def project_odd(h, m):
-            k_banks["odd", h, m] = next_bank("k")
-            multiply(k_banks["odd", h, m][:], latent_codes[m], panels["k", h, 1], True, True)
-
-        def project_even(h, m):
-            k_banks["even", h, m] = next_bank("k")
-            multiply(k_banks["even", h, m][:], latent_codes[m], panels["k", h, 0], True, True)
-
-        def project_v(h, m, part):
-            v_banks[h, m, part] = next_bank("x")
-            multiply(v_banks[h, m, part][:], latent_codes[m], panels["v", h, part], True, True)
+        def project_odd_and_even(h, m):
+            odd_bank[h, m] = next_bank("k")
+            multiply(odd_bank[h, m][:], latent_codes[m], panels["k", h, 1], True, True)
+            even_bank[h, m] = next_bank("k")
+            multiply(even_bank[h, m][:], latent_codes[m], panels["k", h, 0], True, True)
 
         def by_table(out, bank, table, m):
             nc.vector.tensor_tensor(
@@ -358,26 +328,24 @@ def tile_mla_pa_kernel(
             )
 
         def rotate_both(h, m):
-            by_cos[h, m] = stage.tile([P, BANK], F32, name="by_cos", bufs=4)
-            by_table(by_cos[h, m][:], k_banks["both", h, m], cos_raw, m)
+            both_product[h, m] = outs.tile([P, BANK], F32, name="both_product")
+            by_table(both_product[h, m][:], both_bank[h, m], cos, m)
 
-        def rotate_odd(h, m):
-            rest[h, m] = stage.tile([P, 2, BANK], F32, name="rest", bufs=4)
-            by_table(rest[h, m][:, 0], k_banks["odd", h, m], minus_sum, m)
+        def rotate_odd_and_even(h, m):
+            other_products[h, m] = outs.tile([P, 2, BANK], F32, name="other_products")
+            by_table(other_products[h, m][:, 0], odd_bank[h, m], minus_sum, m)
+            by_table(other_products[h, m][:, 1], even_bank[h, m], sin_less_cos, m)
 
-        def rotate_even(h, m):
-            by_table(rest[h, m][:, 1], k_banks["even", h, m], sin_less_cos, m)
-
-        def add_and_store(h, m, engine, parts=1):
+        def add_and_store(h, m, engine, parts):
             k_out = outs.tile([P, HALF_COLS], F32, name="k_out")
             pairs = BANK // parts
             for part in range(parts):
                 now = slice(part * pairs, (part + 1) * pairs)
-                cols = slice(2 * part * pairs, 2 * (part + 1) * pairs)
+                cols = slice(2 * now.start, 2 * now.stop)
                 engine.tensor_tensor(
                     out=k_out[:, cols].rearrange("p (n e) -> p n e", e=2),
-                    in0=by_cos[h, m][:, now].unsqueeze(2).to_broadcast([P, pairs, 2]),
-                    in1=rest[h, m][:, :, now].rearrange("p e n -> p n e"),
+                    in0=both_product[h, m][:, now].unsqueeze(2).to_broadcast([P, pairs, 2]),
+                    in1=other_products[h, m][:, :, now].rearrange("p e n -> p n e"),
                     op=ALU.add,
                 )
                 first = h * HALF_COLS + cols.start
@@ -385,119 +353,58 @@ def tile_mla_pa_kernel(
                     out=k_rows[m * P : (m + 1) * P, first : first + 2 * pairs], in_=k_out[:, cols]
                 )
 
-        v_outs = {}
-
-        def values(h, m, part):
-            if part == 0:
-                v_outs[h, m] = outs.tile([P, HALF_COLS], F32, name="v_out")
-            v_out = v_outs[h, m]
-            scalar_copy(out=v_out[:, part * BANK : (part + 1) * BANK], in_=v_banks[h, m, part][:])
-            if part == 1:
-                nc.scalar.dma_start(
-                    out=v_rows[m * P : (m + 1) * P, h * HALF_COLS : (h + 1) * HALF_COLS], in_=v_out[:]
-                )
-
-        wc = [("c", g, 0) for g in range(PASSES)]
-        up = [(kind, h, part) for h in range(2) for kind, part in (("k", 1), ("k", 0), ("v", 0), ("v", 1))]
-
-        def product(panel, side):
-            regroup_by_product(panel, side)
-
-        def on_vector(panel, side):
-            regroup(panel, side, vector_copy)
-
-        def on_scalar(panel, side):
-            regroup(panel, side, scalar_copy)
-
-        def on_gpsimd(panel, side):
-            grouped = grouped_tile(panel)
+        def values(h, m):
+            v_out = outs.tile([P, HALF_COLS], F32, name="v_out")
             for j in range(2):
-                cols = slice((2 * side + j) * P, (2 * side + j + 1) * P)
-                nc.gpsimd.tensor_scalar(
-                    out=grouped[:, cols, :],
-                    in0=panel_source(panel)[:, :, cols].rearrange("p t c -> p c t"),
-                    scalar1=1.0, scalar2=0.0, op0=ALU.mult, op1=ALU.add,
-                )
+                bank = next_bank("turned x")
+                multiply(bank[:], latent_codes[m], panels["v", h, j], True, True)
+                nc.scalar.copy(out=v_out[:, j * BANK : (j + 1) * BANK], in_=bank[:])
+            nc.scalar.dma_start(
+                out=v_rows[m * P : (m + 1) * P, h * HALF_COLS : (h + 1) * HALF_COLS], in_=v_out[:]
+            )
 
-        units = [(h, m) for h in range(2) for m in range(TILES)]
-        gpsimd_adds = [u for j, u in enumerate(units) if j % 2 == 1 and j >= 3 and j < 14]
-
-        def add(unit):
-            engine = nc.gpsimd if unit in gpsimd_adds else nc.vector
-            add_and_store(*unit, engine, 2 if unit == units[-1] else 1)
-
-        def extra(s, at):
-            for when, function, panel, sides in work:
-                if when == (s, at):
-                    for side in sides:
-                        if side is None:
-                            function(panel)
-                        else:
-                            function(panel, side)
-
-        q = quantise_panel
-        qp = quantise_pair
-        qp = quantise_pair
-        on_vector(wc[0], 0)
+        regroup(("c", 0), slice(0, BANK), nc.vector.tensor_copy)
         turn_tokens(0)
         empty_tokens(0)
-        on_vector(wc[0], 1)
-        product(wc[1], 1)
-        q(wc[0])
-        on_vector(wc[1], 0)
-        product(wc[2], 1)
-        quantise_tokens(0)
-        on_vector(wc[2], 0)
-        product(wc[3], 1)
-        q(wc[1])
-        on_vector(wc[3], 0)
+        quantise_compress(0)
+        for g in range(1, PASSES):
+            regroup(("c", g), second_part, nc.scalar.copy)
+            regroup(("c", g), first_part, nc.vector.tensor_copy)
+            if g == 1:
+                quantise_tokens(0)
+            else:
+                quantise_compress(g - 1)
         spread_gain()
         turn_tokens(1)
-        q(wc[2])
-        q(wc[3])
+        quantise_compress(PASSES - 1)
         compress(0)
         empty_tokens(1)
-        sum_up_squares(0)
-        take_root(0)
+        sum_squares(0)
+        invert_rms(0)
 
-        work = [
-            ((1, 1), on_vector, up[0], (0,)),
-            ((1, 1), on_gpsimd, up[0], (1,)),
-            ((2, 1), on_vector, up[1], (0,)),
-            ((2, 1), on_gpsimd, up[1], (1,)),
-            ((3, 0), qp, up[0], (None,)),
-            ((3, 1), on_vector, up[2], (0,)),
-            ((3, 1), on_gpsimd, up[2], (1,)),
-            ((4, 1), on_vector, up[3], (0,)),
-            ((4, 1), on_gpsimd, up[3], (1,)),
-            ((6, 0), qp, up[2], (None,)),
-            ((6, 2), on_scalar, up[4], (0,)),
-            ((7, 2), on_scalar, up[4], (1,)),
-            ((8, 2), on_scalar, up[5], (0,)),
-            ((9, 2), on_scalar, up[5], (1,)),
-            ((10, 2), on_scalar, up[6], (0,)),
-            ((11, 2), on_scalar, up[6], (1,)),
-            ((12, 2), on_scalar, up[7], (0,)),
-            ((13, 2), on_scalar, up[7], (1,)),
-            ((12, 3), qp, up[4], (None,)),
-            ((14, 3), qp, up[6], (None,)),
-
+        early = [("k", 0, 1), ("k", 0, 0), ("v", 0, 0), ("v", 0, 1)]
+        late = [
+            (panel, cols)
+            for panel in (("k", 1, 1), ("k", 1, 0), ("v", 1, 0), ("v", 1, 1))
+            for cols in (first_part, second_part)
         ]
-        first_unit = 7
-        for s in range(1, first_unit + len(units) + 1):
-            j = s - first_unit
+        units = [(h, m) for h in range(2) for m in range(TILES)]
+        gpsimd_units = [3, 5, 7, 9, 11, 13]
+
+        for s in range(1, FIRST_UNIT_STEP + len(units) + 1):
+            j = s - FIRST_UNIT_STEP
             unit = units[j] if 0 <= j < len(units) else None
-            older = units[j - 1] if 1 <= j <= len(units) else None
             if s == TILES + 2:
-                rings["k"].extend(rings["s"] + rings["c"])
+                rings["k"].extend(rings["turned"] + rings["c"])
             if s + 1 < TILES:
                 turn_tokens(s + 1)
             if s < TILES:
                 quantise_tokens(s)
-            if unit is None and s - 1 < TILES:
-                invert(s - 1)
-            extra(s, 0)
-            if 0 <= s - 2 < TILES:
+            if s == 3:
+                quantise_up("k", 0)
+            if s == 5:
+                quantise_up("v", 0)
+            if 2 <= s < TILES + 2:
                 quantise_latent(s - 2)
             if s + 1 < TILES:
                 empty_tokens(s + 1)
@@ -505,33 +412,34 @@ def tile_mla_pa_kernel(
                 project_both(*unit)
             if s < TILES:
                 compress(s)
-            extra(s, 1)
-            if unit and s - 1 < TILES:
-                invert(s - 1)
+            if s <= len(early):
+                regroup(early[s - 1], first_part, nc.vector.tensor_copy)
+                regroup_on_gpsimd(early[s - 1], second_part)
             if unit:
-                project_odd(*unit)
-                project_even(*unit)
+                project_odd_and_even(*unit)
                 rotate_both(*unit)
-            if s - 1 < TILES:
+            if s < TILES + 1:
                 normalise(s - 1)
                 turn_latent(s - 1)
             if unit:
-                rotate_odd(*unit)
-                rotate_even(*unit)
-            if older and older not in gpsimd_adds:
-                add(older)
-            extra(s, 3)
-            if unit and unit in gpsimd_adds:
-                add(unit)
+                rotate_odd_and_even(*unit)
+            if 1 <= j and j - 1 not in gpsimd_units:
+                add_and_store(*units[j - 1], nc.vector, 2 if j == len(units) else 1)
+            if s == SECOND_HALF_STEP + 4:
+                quantise_up("k", 1)
+            if s == SECOND_HALF_STEP + 8:
+                quantise_up("v", 1)
+            if j in gpsimd_units:
+                add_and_store(*unit, nc.gpsimd, 1)
             if s < TILES:
-                sum_up_squares(s)
-            if s - 1 < TILES:
+                sum_squares(s)
+            if s < TILES + 1:
                 empty_latent(s - 1)
             if s < TILES:
-                take_root(s)
-            for vu in [u for k, u in enumerate(units) if (k + 1 if k < 8 else k) == j]:
-                project_v(*vu, 0)
-                values(*vu, 0)
-                project_v(*vu, 1)
-                values(*vu, 1)
-            extra(s, 2)
+                invert_rms(s)
+            if 1 <= j <= TILES:
+                values(*units[j - 1])
+            if TILES <= j < len(units):
+                values(*unit)
+            if 0 <= s - SECOND_HALF_STEP < len(late):
+                regroup(*late[s - SECOND_HALF_STEP], nc.scalar.copy)

@@ -28,6 +28,7 @@ HEADS = HALF_COLS // HEAD
 POSITIONS = 256
 PHASES = POSITIONS // P
 EPS = 1e-6
+WARM_UPS = 32
 
 FLOPS = 2 * TOKENS * D_MODEL * RANK + 2 * 2 * TOKENS * RANK * OUT_COLS
 
@@ -362,6 +363,10 @@ def tile_mla_pa_kernel(
             nc.scalar.dma_start(
                 out=v_rows[m * P : (m + 1) * P, h * HALF_COLS : (h + 1) * HALF_COLS], in_=v_out[:]
             )
+
+        warm_bank = next_bank("k")
+        for n in range(WARM_UPS):
+            nc.tensor.matmul(warm_bank[:, :P], lhsT=ones[:], rhs=ones[:], start=True, stop=True)
 
         regroup(("c", 0), slice(0, BANK), nc.vector.tensor_copy)
         turn_tokens(0)

from contextlib import ExitStack

import concourse.mybir as mybir
from concourse.masks import make_identity

FP8X4 = mybir.dt.float8_e4m3fn_x4
BF16 = mybir.dt.bfloat16
F32 = mybir.dt.float32
U32 = mybir.dt.uint32
U8 = mybir.dt.uint8
ALU = mybir.AluOpType
ACT = mybir.ActivationFunctionType

P = 128
PACK = 4
K_PASS = P * PACK
TOKENS = 1024
TILES = TOKENS // P
D_MODEL = 2048
PASSES = D_MODEL // K_PASS
RANK = 512
OUT_COLS = 2048
BANK = 512
HALF_COLS = OUT_COLS // 2
HEAD = 128
PAIRS = HEAD // 2
HEADS = HALF_COLS // HEAD
POSITIONS = 256
PHASES = POSITIONS // P
EPS = 1e-6
WARM_UPS = 32

FLOPS = 2 * TOKENS * D_MODEL * RANK + 2 * 2 * TOKENS * RANK * OUT_COLS

FIRST_UNIT_STEP = 7
SECOND_HALF_STEP = 6


def tile_mla_pa_kernel(
    tc, x, freqs_cos, freqs_sin, w_kv_compress, kv_norm_w, w_k_up, w_v_up, out_0, out_1
):
    nc = tc.nc
    x_rows = x.flatten_outer_dims()
    k_rows = out_0.rearrange("b s h d -> (b s) (h d)")
    v_rows = out_1.rearrange("b s h d -> (b s) (h d)")

    with ExitStack() as stack:
        keep = stack.enter_context(tc.tile_pool(name="keep", bufs=1))
        stage = stack.enter_context(tc.tile_pool(name="stage", bufs=3))
        outs = stack.enter_context(tc.tile_pool(name="outs", bufs=4))
        psum = stack.enter_context(tc.psum_pool(name="psum", bufs=1))
        stack.enter_context(tc.manual_schedule())

        rings = {"k": [0, 1, 2], "turned": [3], "turned x": [4, 5], "c": [6, 7]}

        def next_bank(use):
            number = rings[use].pop(0)
            rings[use].append(number)
            return psum.tile([P, BANK], F32, name="bank%d" % number)

        eps = keep.tile([P, 1], F32)
        nc.vector.memset(eps[:], EPS)
        table_warmer = keep.tile([P, 1], F32)
        nc.scalar.activation(out=table_warmer[:], in_=eps[:], func=ACT.Abs_reciprocal_sqrt)
        ident = keep.tile([P, P], F32)
        make_identity(nc, ident[:])
        ones = keep.tile([P, P], BF16)
        nc.vector.memset(ones[:], 1.0)
        gain_row = keep.tile([P, RANK], BF16)
        nc.vector.memset(gain_row[:], 0.0)

        x_raw = {}
        wc_raw = {}
        up_raw = {}

        def load_tokens(m):
            x_raw[m] = keep.tile([P, D_MODEL], BF16, name="x_raw%d" % m)
            nc.sync.dma_start(out=x_raw[m][:], in_=x_rows[m * P : (m + 1) * P, :])

        def load_compress(g):
            wc_raw[g] = keep.tile([P, PACK, RANK], BF16, name="wc_raw%d" % g)
            nc.sync.dma_start(
                out=wc_raw[g][:].rearrange("p (u e) c -> p u e c", e=2),
                in_=w_kv_compress[g * K_PASS : (g + 1) * K_PASS, :].rearrange(
                    "(u q e) c -> q u e c", u=2, e=2
                ),
            )

        def load_up(kind, weight, h):
            up_raw[kind, h] = keep.tile([P, PACK, HALF_COLS], BF16, name="%s_raw%d" % (kind, h))
            for u in range(2):
                nc.sync.dma_start(
                    out=up_raw[kind, h][:, 2 * u : 2 * u + 2, :],
                    in_=weight[
                        u * 2 * P : (u + 1) * 2 * P, h * HALF_COLS : (h + 1) * HALF_COLS
                    ].rearrange("(q e) c -> q e c", e=2),
                )

        load_compress(0)
        load_tokens(0)
        for g in range(1, PASSES):
            load_compress(g)
        load_tokens(1)
        nc.sync.dma_start(out=gain_row[0:1, :], in_=kv_norm_w.unsqueeze(0))
        load_tokens(2)
        cos = keep.tile([P, PHASES, PAIRS], BF16)
        nc.sync.dma_start(out=cos[:], in_=freqs_cos.rearrange("(a p) i -> p a i", p=P))
        sin = keep.tile([P, PHASES, PAIRS], BF16)
        nc.sync.dma_start(out=sin[:], in_=freqs_sin.rearrange("(a p) i -> p a i", p=P))
        load_up("k", w_k_up, 0)
        load_tokens(3)
        load_up("v", w_v_up, 0)
        for m in range(4, TILES):
            load_tokens(m)
        load_up("k", w_k_up, 1)
        load_up("v", w_v_up, 1)

        sin_less_cos = keep.tile([P, PHASES, PAIRS], F32)
        nc.gpsimd.tensor_tensor(out=sin_less_cos[:], in0=sin[:], in1=cos[:], op=ALU.subtract)
        cos_plus_sin = keep.tile([P, PHASES, PAIRS], F32)
        nc.gpsimd.tensor_tensor(out=cos_plus_sin[:], in0=sin[:], in1=cos[:], op=ALU.add)
        minus_sum = keep.tile([P, PHASES, PAIRS], F32)
        nc.gpsimd.tensor_scalar(
            out=minus_sum[:], in0=cos_plus_sin[:], scalar1=-1.0, scalar2=0.0,
            op0=ALU.mult, op1=ALU.add,
        )

        grouped = {}
        grouped_pair = {}
        panels = {}

        def panel_source(panel):
            if panel[0] == "c":
                return wc_raw[panel[1]][:]
            kind, h, j = panel
            if kind == "v":
                return up_raw["v", h][:, :, j * BANK : (j + 1) * BANK]
            return up_raw["k", h][:].rearrange("p t (n e) -> p t n e", e=2)[:, :, :, j]

        def grouped_tile(panel):
            if panel not in grouped:
                if panel[0] == "c":
                    grouped[panel] = stage.tile(
                        [P, BANK, PACK], BF16, name="grouped", align_bytes=64
                    )[:]
                else:
                    pair = stage.tile(
                        [P, 2, BANK, PACK], BF16, name="grouped_pair", align_bytes=64, bufs=2
                    )
                    grouped_pair[panel[:2]] = pair
                    for j in range(2):
                        grouped[panel[0], panel[1], j] = pair[:, j]
            return grouped[panel]

        first_part, second_part = slice(0, BANK // 2), slice(BANK // 2, BANK)

        def regroup(panel, cols, copy):
            copy(
                out=grouped_tile(panel)[:, cols, :].rearrange("p (c i) t -> p c t i", i=4),
                in_=panel_source(panel)[:, :, cols].rearrange("p t (c i) -> p c t i", i=4),
            )

        def regroup_on_gpsimd(panel, cols):
            middle = (cols.start + cols.stop) // 2
            for now in (slice(cols.start, middle), slice(middle, cols.stop)):
                nc.gpsimd.tensor_scalar(
                    out=grouped_tile(panel)[:, now, :],
                    in0=panel_source(panel)[:, :, now].rearrange("p t c -> p c t"),
                    scalar1=1.0, scalar2=0.0, op0=ALU.mult, op1=ALU.add,
                )

        def quantise_compress(g):
            codes = keep.tile([P, BANK], U32, name="codes_c%d" % g, align_bytes=64)
            scales = keep.tile([P, BANK], U8, name="scales_c%d" % g, align_bytes=64)
            nc.vector.quantize_mx(
                out=codes[:].bitcast(FP8X4), scales=scales[:],
                in_=grouped["c", g].rearrange("p c t -> p (c t)"),
            )
            panels["c", g] = (codes[:], scales[:])

        def quantise_up(kind, h):
            codes = keep.tile([P, 2, BANK], U32, name="codes_%s%d" % (kind, h), align_bytes=64)
            scales = keep.tile([P, 2, BANK], U8, name="scales_%s%d" % (kind, h), align_bytes=64)
            nc.vector.quantize_mx(
                out=codes[:].rearrange("p j c -> p (j c)").bitcast(FP8X4),
                scales=scales[:].rearrange("p j c -> p (j c)"),
                in_=grouped_pair[kind, h][:].rearrange("p j c t -> p (j c t)"),
            )
            for j in range(2):
                panels[kind, h, j] = (codes[:, j], scales[:, j])

        def multiply(out, left, right, start, stop):
            nc.tensor.matmul_mx(
                out=out,
                lhsT=left[0].bitcast(FP8X4),
                lhsT_scale=left[1],
                rhs=right[0].bitcast(FP8X4),
                rhs_scale=right[1],
                start=start,
                stop=stop,
            )

        x_banks = {}
        x_grouped = {}
        x_codes = {}

        def turn_tokens(m):
            words = x_raw[m][:].bitcast(F32)
            x_banks[m] = []
            for b in range(2):
                bank = next_bank("turned x")
                for j in range(4):
                    first = (4 * b + j) * P
                    nc.tensor.transpose(
                        bank[:, j * P : (j + 1) * P], words[:, first : first + P], ident[:]
                    )
                x_banks[m].append(bank)

        def empty_tokens(m):
            x_grouped[m] = stage.tile([P, PASSES * P * PACK], BF16, name="x_grouped", align_bytes=64)
            words = x_grouped[m][:].bitcast(F32).rearrange("p (b g r u) -> p b g r u", b=2, g=2, u=2)
            for b in range(2):
                nc.scalar.copy(
                    out=words[:, b],
                    in_=x_banks[m][b][:].rearrange("p (g u r) -> p g r u", g=2, u=2),
                )

        def quantise_tokens(m):
            codes = stage.tile([P, PASSES, P], U32, name="x_codes", align_bytes=64)
            scales = stage.tile([P, PASSES, P], U8, name="x_scales", align_bytes=64)
            nc.vector.quantize_mx(
                out=codes[:].rearrange("p g r -> p (g r)").bitcast(FP8X4),
                scales=scales[:].rearrange("p g r -> p (g r)"),
                in_=x_grouped[m][:],
            )
            x_codes[m] = (codes, scales)

        c_banks = {}
        square_sums = {}
        inverse_rms = {}
        latents = {}
        gain = keep.tile([P, RANK], F32)

        def compress(m):
            codes, scales = x_codes[m]
            c_banks[m] = next_bank("c")
            for g in range(PASSES):
                multiply(
                    c_banks[m][:], (codes[:, g, :], scales[:, g, :]), panels["c", g],
                    g == 0, g == PASSES - 1,
                )

        def sum_squares(m):
            squares = stage.tile([P, RANK], BF16, name="squares")
            square_sums[m] = stage.tile([P, 1], F32, name="square_sums")
            nc.scalar.activation(
                out=squares[:], in_=c_banks[m][:], func=ACT.Square, accum_out=square_sums[m][:]
            )

        def invert_rms(m):
            inverse_rms[m] = stage.tile([P, 1], F32, name="inverse_rms")
            nc.scalar.activation(
                out=inverse_rms[m][:], in_=square_sums[m][:], func=ACT.Abs_reciprocal_sqrt,
                bias=eps[:], scale=1.0 / RANK,
            )

        def spread_gain():
            bank = next_bank("k")
            nc.tensor.matmul(bank[:], lhsT=ones[:], rhs=gain_row[:], start=True, stop=True)
            nc.scalar.copy(out=gain[:], in_=bank[:])

        def normalise(m):
            latents[m] = stage.tile([P, RANK], BF16, name="latent")
            nc.vector.scalar_tensor_tensor(
                out=latents[m][:], in0=c_banks[m][:], scalar=inverse_rms[m][:], in1=gain[:],
                op0=ALU.mult, op1=ALU.mult,
            )

        latent_banks = {}
        latent_grouped = {}
        latent_codes = {}

        def turn_latent(m):
            words = latents[m][:].bitcast(F32)
            latent_banks[m] = next_bank("turned")
            for u in range(2):
                nc.tensor.transpose(
                    latent_banks[m][:, u * P : (u + 1) * P], words[:, u * P : (u + 1) * P], ident[:]
                )

        def empty_latent(m):
            latent_grouped[m] = stage.tile([P, P * PACK], BF16, name="latent_grouped", align_bytes=64)
            nc.scalar.copy(
                out=latent_grouped[m][:].bitcast(F32).rearrange("p (r u) -> p r u", u=2),
                in_=latent_banks[m][:, : 2 * P].rearrange("p (u r) -> p r u", u=2),
            )

        def quantise_latent(m):
            codes = keep.tile([P, P], U32, name="latent_codes%d" % m, align_bytes=64)
            scales = keep.tile([P, P], U8, name="latent_scales%d" % m, align_bytes=64)
            nc.vector.quantize_mx(
                out=codes[:].bitcast(FP8X4), scales=scales[:], in_=latent_grouped[m][:]
            )
            latent_codes[m] = (codes[:], scales[:])

        both_bank = {}
        odd_bank = {}
        even_bank = {}
        both_product = {}
        other_products = {}

        def project_both(h, m):
            both_bank[h, m] = next_bank("k")
            multiply(both_bank[h, m][:], latent_codes[m], panels["k", h, 1], True, False)
            multiply(both_bank[h, m][:], latent_codes[m], panels["k", h, 0], False, True)

        def project_odd_and_even(h, m):
            odd_bank[h, m] = next_bank("k")
            multiply(odd_bank[h, m][:], latent_codes[m], panels["k", h, 1], True, True)
            even_bank[h, m] = next_bank("k")
            multiply(even_bank[h, m][:], latent_codes[m], panels["k", h, 0], True, True)

        def by_table(out, bank, table, m):
            nc.vector.tensor_tensor(
                out=out.rearrange("p (h i) -> p h i", h=HEADS),
                in0=bank[:].rearrange("p (h i) -> p h i", h=HEADS),
                in1=table[:, m % PHASES].unsqueeze(1).to_broadcast([P, HEADS, PAIRS]),
                op=ALU.mult,
            )

        def rotate_both(h, m):
            both_product[h, m] = outs.tile([P, BANK], F32, name="both_product")
            by_table(both_product[h, m][:], both_bank[h, m], cos, m)

        def rotate_odd_and_even(h, m):
            other_products[h, m] = outs.tile([P, 2, BANK], F32, name="other_products")
            by_table(other_products[h, m][:, 0], odd_bank[h, m], minus_sum, m)
            by_table(other_products[h, m][:, 1], even_bank[h, m], sin_less_cos, m)

        def add_and_store(h, m, engine, parts):
            k_out = outs.tile([P, HALF_COLS], F32, name="k_out")
            pairs = BANK // parts
            for part in range(parts):
                now = slice(part * pairs, (part + 1) * pairs)
                cols = slice(2 * now.start, 2 * now.stop)
                engine.tensor_tensor(
                    out=k_out[:, cols].rearrange("p (n e) -> p n e", e=2),
                    in0=both_product[h, m][:, now].unsqueeze(2).to_broadcast([P, pairs, 2]),
                    in1=other_products[h, m][:, :, now].rearrange("p e n -> p n e"),
                    op=ALU.add,
                )
                first = h * HALF_COLS + cols.start
                nc.sync.dma_start(
                    out=k_rows[m * P : (m + 1) * P, first : first + 2 * pairs], in_=k_out[:, cols]
                )

        def values(h, m):
            v_out = outs.tile([P, HALF_COLS], F32, name="v_out")
            for j in range(2):
                bank = next_bank("turned x")
                multiply(bank[:], latent_codes[m], panels["v", h, j], True, True)
                nc.scalar.copy(out=v_out[:, j * BANK : (j + 1) * BANK], in_=bank[:])
            nc.scalar.dma_start(
                out=v_rows[m * P : (m + 1) * P, h * HALF_COLS : (h + 1) * HALF_COLS], in_=v_out[:]
            )

        warm_bank = next_bank("k")
        for n in range(WARM_UPS):
            nc.tensor.matmul(warm_bank[:, :P], lhsT=ones[:], rhs=ones[:], start=True, stop=True)

        regroup(("c", 0), slice(0, BANK), nc.vector.tensor_copy)
        turn_tokens(0)
        empty_tokens(0)
        quantise_compress(0)
        for g in range(1, PASSES):
            regroup(("c", g), second_part, nc.scalar.copy)
            regroup(("c", g), first_part, nc.vector.tensor_copy)
            if g == 1:
                quantise_tokens(0)
            else:
                quantise_compress(g - 1)
        spread_gain()
        turn_tokens(1)
        quantise_compress(PASSES - 1)
        compress(0)
        empty_tokens(1)
        sum_squares(0)
        invert_rms(0)

        early = [("k", 0, 1), ("k", 0, 0), ("v", 0, 0), ("v", 0, 1)]
        late = [
            (panel, cols)
            for panel in (("k", 1, 1), ("k", 1, 0), ("v", 1, 0), ("v", 1, 1))
            for cols in (first_part, second_part)
        ]
        units = [(h, m) for h in range(2) for m in range(TILES)]
        gpsimd_units = [3, 5, 7, 9, 11, 13]

        for s in range(1, FIRST_UNIT_STEP + len(units) + 1):
            j = s - FIRST_UNIT_STEP
            unit = units[j] if 0 <= j < len(units) else None
            if s == TILES + 2:
                rings["k"].extend(rings["turned"] + rings["c"])
            if s + 1 < TILES:
                turn_tokens(s + 1)
            if s < TILES:
                quantise_tokens(s)
            if s == 3:
                quantise_up("k", 0)
            if s == 5:
                quantise_up("v", 0)
            if 2 <= s < TILES + 2:
                quantise_latent(s - 2)
            if s + 1 < TILES:
                empty_tokens(s + 1)
            if unit:
                project_both(*unit)
            if s < TILES:
                compress(s)
            if s <= len(early):
                regroup(early[s - 1], first_part, nc.vector.tensor_copy)
                regroup_on_gpsimd(early[s - 1], second_part)
            if unit:
                project_odd_and_even(*unit)
                rotate_both(*unit)
            if s < TILES + 1:
                normalise(s - 1)
                turn_latent(s - 1)
            if unit:
                rotate_odd_and_even(*unit)
            if 1 <= j and j - 1 not in gpsimd_units:
                add_and_store(*units[j - 1], nc.vector, 2 if j == len(units) else 1)
            if s == SECOND_HALF_STEP + 4:
                quantise_up("k", 1)
            if s == SECOND_HALF_STEP + 8:
                quantise_up("v", 1)
            if j in gpsimd_units:
                add_and_store(*unit, nc.gpsimd, 1)
            if s < TILES:
                sum_squares(s)
            if s < TILES + 1:
                empty_latent(s - 1)
            if s < TILES:
                invert_rms(s)
            if 1 <= j <= TILES:
                values(*units[j - 1])
            if TILES <= j < len(units):
                values(*unit)
            if 0 <= s - SECOND_HALF_STEP < len(late):
                regroup(*late[s - SECOND_HALF_STEP], nc.scalar.copy)
